import numpy as np
import ml_dtypes


def mxq(x, axis, fmt="e4m3"):
    dtype, down = {"e4m3": (ml_dtypes.float8_e4m3fn, 7), "e5m2": (ml_dtypes.float8_e5m2, 14)}[fmt]
    v = np.moveaxis(np.asarray(x, np.float32).astype(ml_dtypes.bfloat16).astype(np.float64), axis, -1)
    blocks = v.reshape(v.shape[:-1] + (-1, 32))
    amax = np.abs(blocks).max(-1, keepdims=True)
    byte = np.maximum(np.where(amax > 0, np.frexp(amax)[1] - 1 + 127, 0) - down, 1)
    scale = np.exp2(byte - 127.0)
    codes = (blocks / scale).astype(np.float32).astype(dtype).astype(np.float64)
    return np.moveaxis((codes * scale).reshape(v.shape), -1, axis)


WIDE = False


def mx_kscale(k):
    if not WIDE:
        return np.ones(k)
    levels = np.array([10, -10, 5, -5, 0])
    a = np.random.permutation(np.resize(levels, k // 512 * 4)).reshape(k // 512, 4)
    idx = np.arange(k)
    return np.exp2(a[idx // 512, idx % 128 // 32])


BF16 = ml_dtypes.bfloat16


def bf(x):
    return np.asarray(x, np.float32).astype(BF16)


def f64(x):
    return np.asarray(x).astype(np.float64)


B, T, N, D, H = 1, 3, 512, 1024, 8
HD = D // H


def split_heads(x):
    return np.moveaxis(x.reshape(B, T, N, H, HD), 3, 0).reshape(H * B, T, N, HD)


def merge_heads(x):
    return np.moveaxis(x.reshape(H, B, T, N, HD), 0, 3).reshape(B, T, N, D)


def setup_inputs():
    s = mx_kscale(D)
    return {"q_heads": bf(np.random.standard_normal((H * B, T, N, HD)) * 1.5),
            "k_heads": bf(np.random.standard_normal((H * B, T, N, HD)) * 1.6),
            "value": bf(np.random.standard_normal((B, T, N, D)) * s),
            "Wv": bf(np.random.standard_normal((D, D)) * 1.5 / np.sqrt(D) / s),
            "bv": bf(np.random.standard_normal(D) * 0.2),
            "dyn": bf(np.random.standard_normal((H * B, T, N, N)) * 0.6),
            "h_gcn": bf(np.maximum(np.random.standard_normal((B, T, N, D)), 0.0))}


def reference(q_heads, k_heads, value, Wv, bv, dyn, h_gcn):
    v2 = split_heads((mxq(f64(value), 3, "e4m3") @ mxq(f64(Wv), 1, "e4m3").T) + f64(bv))
    score = f64(q_heads) @ f64(k_heads).transpose(0, 1, 3, 2) / np.sqrt(HD)
    g = score * f64(dyn)
    e = np.exp(g - g.max(-1, keepdims=True))
    o = (mxq(e, 3, "e4m3") @ mxq(v2, 2, "e4m3")) / e.sum(-1, keepdims=True)
    return 0.5 * f64(h_gcn) + 0.5 * merge_heads(np.tanh(o))

@@ -1,0 +1,321 @@
+from contextlib import ExitStack
+import math
+
+import concourse.mybir as mybir
+from concourse.masks import make_identity
+
+F32 = mybir.dt.float32
+BF16 = mybir.dt.bfloat16
+U32 = mybir.dt.uint32
+U8 = mybir.dt.uint8
+FP8X4 = mybir.dt.float8_e4m3fn_x4
+ALU = mybir.AluOpType
+ACT = mybir.ActivationFunctionType
+AX = mybir.AxisListType
+
+P = 128
+PACK = 4
+STEPS = 3
+HEADS = 8
+NODES = 512
+FEATURES = 1024
+HEAD_DIM = FEATURES // HEADS
+NODE_TILES = NODES // P
+FEATURE_PASSES = FEATURES // (P * PACK)
+SCORE_SCALE = 1.0 / math.sqrt(HEAD_DIM)
+
+FLOPS = 2 * STEPS * NODES * FEATURES * FEATURES + 2 * (2 * STEPS * HEADS * NODES * NODES * HEAD_DIM)
+
+
+SLICES = STEPS * HEADS
+
+
+def tile_gatedspatialattentionlayer_pb_t_kernel(
+    tc, q_heads, k_heads, value, Wv, bv, dyn, h_gcn, out
+):
+    nc = tc.nc
+    with ExitStack() as ctx:
+        ctx.enter_context(tc.manual_schedule())
+        const = ctx.enter_context(tc.tile_pool(name="const", bufs=1))
+        project = ctx.enter_context(tc.tile_pool(name="project", bufs=STEPS))
+        loads = ctx.enter_context(tc.tile_pool(name="loads", bufs=3))
+        work = ctx.enter_context(tc.tile_pool(name="work", bufs=2))
+        psum = ctx.enter_context(tc.psum_pool(name="psum", bufs=1))
+
+        ident_bf16 = const.tile([P, P], BF16)
+        make_identity(nc, ident_bf16[:])
+        ident_f32 = const.tile([P, P], F32)
+        make_identity(nc, ident_f32[:])
+
+        live = {}
+
+        w_rows = const.tile([P, HEADS, FEATURES], BF16)
+        w_grouped = const.tile([P, HEADS, FEATURE_PASSES, P, PACK], BF16, align_bytes=64)
+        w_codes = const.tile([P, HEADS, FEATURE_PASSES, P], U32, align_bytes=64)
+        w_scales = const.tile([P, HEADS, FEATURE_PASSES, P], U8, align_bytes=64)
+        bias_rows = const.tile([P, FEATURES], BF16)
+        v_codes = const.tile([P, STEPS, HEADS, HEAD_DIM], U32, align_bytes=64)
+        v_scales = const.tile([P, STEPS, HEADS, HEAD_DIM], U8, align_bytes=64)
+        half = HEADS // 2
+
+        def load_projection_operands():
+            w_view = Wv.rearrange("(h r) f -> r h f", r=P)
+            for c in range(2):
+                heads = slice(c * half, (c + 1) * half)
+                nc.sync.dma_start(out=w_rows[:, heads, :], in_=w_view[:, heads, :])
+            nc.sync.dma_start(out=bias_rows[:], in_=bv.partition_broadcast(P))
+            for t in range(STEPS):
+                x_rows = project.tile([P, NODE_TILES, FEATURES], BF16)
+                nc.sync.dma_start(out=x_rows[:], in_=value[0, t].rearrange("(p x) f -> p x f", x=NODE_TILES))
+                live["x_rows", t] = x_rows
+
+        def features_to_partitions(rows, grouped):
+            words = rows.bitcast(F32)
+            flipped = psum.tile([P, FEATURE_PASSES, 2, P], F32, tag="e_flip", bufs=2)
+            for g in range(FEATURE_PASSES):
+                for u in range(2):
+                    first = (2 * g + u) * P
+                    nc.tensor.transpose(
+                        out=flipped[:, g, u, :], in_=words[:, first : first + P], identity=ident_f32[:]
+                    )
+            nc.scalar.copy(out=grouped.bitcast(F32), in_=flipped[:].rearrange("p g u r -> p g r u"))
+
+        def flip_projection_operands():
+            for h in range(HEADS):
+                features_to_partitions(w_rows[:, h, :], w_grouped[:, h])
+            for t in range(STEPS):
+                x_grouped = project.tile([P, NODE_TILES, FEATURE_PASSES, P, PACK], BF16, align_bytes=64)
+                for x in range(NODE_TILES):
+                    features_to_partitions(live["x_rows", t][:, x, :], x_grouped[:, x])
+                live["x_grouped", t] = x_grouped
+
+        def project_values():
+            for c in range(2):
+                heads = slice(c * half, (c + 1) * half)
+                nc.vector.quantize_mx(
+                    out=w_codes[:, heads].rearrange("p h g r -> p (h g r)").bitcast(FP8X4),
+                    scales=w_scales[:, heads].rearrange("p h g r -> p (h g r)"),
+                    in_=w_grouped[:, heads].rearrange("p h g r j -> p (h g r j)"),
+                )
+            for t in range(STEPS):
+                x_codes = project.tile([P, NODE_TILES, FEATURE_PASSES, P], U32, align_bytes=64)
+                x_scales = project.tile([P, NODE_TILES, FEATURE_PASSES, P], U8, align_bytes=64)
+                nc.vector.quantize_mx(
+                    out=x_codes[:].rearrange("p x g r -> p (x g r)").bitcast(FP8X4),
+                    scales=x_scales[:].rearrange("p x g r -> p (x g r)"),
+                    in_=live["x_grouped", t][:].rearrange("p x g r j -> p (x g r j)"),
+                )
+                live["x_codes", t] = x_codes
+                live["x_scales", t] = x_scales
+            for t in range(STEPS):
+                x_codes = live["x_codes", t]
+                x_scales = live["x_scales", t]
+                v_grouped = project.tile([P, HEADS, HEAD_DIM, PACK], BF16, align_bytes=64, bufs=2)
+                for h in range(HEADS):
+                    v_sums = psum.tile([P, PACK, HEAD_DIM], F32, tag="scores", bufs=NODE_TILES)
+                    for x in range(NODE_TILES):
+                        place = 2 * (x % 2) + x // 2
+                        for g in range(FEATURE_PASSES):
+                            nc.tensor.matmul_mx(
+                                out=v_sums[:, place, :],
+                                lhsT=x_codes[:, x, g, :].bitcast(FP8X4),
+                                lhsT_scale=x_scales[:, x, g, :],
+                                rhs=w_codes[:, h, g, :].bitcast(FP8X4),
+                                rhs_scale=w_scales[:, h, g, :],
+                                start=(g == 0),
+                                stop=(g == FEATURE_PASSES - 1),
+                            )
+                    nc.vector.tensor_tensor(
+                        out=v_grouped[:, h],
+                        in0=v_sums[:].rearrange("p j d -> p d j"),
+                        in1=bias_rows[:, h * HEAD_DIM : (h + 1) * HEAD_DIM]
+                        .unsqueeze(2)
+                        .to_broadcast([P, HEAD_DIM, PACK]),
+                        op=ALU.add,
+                    )
+                nc.vector.quantize_mx(
+                    out=v_codes[:, t].rearrange("p h d -> p (h d)").bitcast(FP8X4),
+                    scales=v_scales[:, t].rearrange("p h d -> p (h d)"),
+                    in_=v_grouped[:].rearrange("p h d j -> p (h d j)"),
+                )
+
+        def load_qk(s):
+            t, h = s // HEADS, s % HEADS
+            q_rows = loads.tile([P, NODE_TILES, HEAD_DIM], BF16)
+            nc.sync.dma_start(out=q_rows[:], in_=q_heads[h, t].rearrange("(p i) d -> p i d", i=NODE_TILES))
+            k_rows = loads.tile([P, 2, 2, HEAD_DIM], BF16)
+            nc.sync.dma_start(out=k_rows[:], in_=k_heads[h, t].rearrange("(a p u) d -> p a u d", a=2, u=2))
+            live["q_rows", s], live["k_rows", s] = q_rows, k_rows
+
+        def load_gate(s):
+            t, h = s // HEADS, s % HEADS
+            dyn_rows = loads.tile([P, NODE_TILES, NODES], BF16, bufs=4)
+            nc.sync.dma_start(out=dyn_rows[:], in_=dyn[h, t].rearrange("(p i) m -> p i m", i=NODE_TILES))
+            h_rows = loads.tile([P, NODE_TILES, HEAD_DIM], BF16, bufs=6)
+            nc.sync.dma_start(
+                out=h_rows[:],
+                in_=h_gcn[0, t].rearrange("(p i) f -> p i f", i=NODE_TILES)[:, :, h * HEAD_DIM : (h + 1) * HEAD_DIM],
+            )
+            live["dyn_rows", s], live["h_rows", s] = dyn_rows, h_rows
+
+        def flip_qk(s):
+            qk_flipped = psum.tile([P, 2 * NODE_TILES, P], BF16, tag="flip")
+            for i in range(NODE_TILES):
+                nc.tensor.transpose(out=qk_flipped[:, i, :], in_=live["q_rows", s][:, i, :], identity=ident_bf16[:])
+            for u in range(2):
+                for a in range(2):
+                    nc.tensor.transpose(
+                        out=qk_flipped[:, NODE_TILES + 2 * u + a, :],
+                        in_=live["k_rows", s][:, a, u, :],
+                        identity=ident_bf16[:],
+                    )
+            live["qk_flipped", s] = qk_flipped
+
+        def keep_qk(s):
+            qk_t = work.tile([P, 2 * NODE_TILES, P], BF16, bufs=3)
+            nc.scalar.copy(out=qk_t[:], in_=live["qk_flipped", s][:])
+            live["qk_t", s] = qk_t
+
+        def score(s):
+            qk_t = live["qk_t", s]
+            for i in range(NODE_TILES):
+                scores = psum.tile([P, NODES], F32, tag="scores", bufs=NODE_TILES)
+                nc.tensor.matmul(
+                    out=scores[:],
+                    lhsT=qk_t[:, i, :],
+                    rhs=qk_t[:, NODE_TILES:, :].rearrange("p j c -> p (j c)"),
+                    start=True,
+                    stop=True,
+                )
+                live["scores", s, i] = scores
+
+        def gate(s):
+            gated = work.tile([P, NODE_TILES, NODES], F32)
+            for i in range(NODE_TILES):
+                nc.vector.scalar_tensor_tensor(
+                    out=gated[:, i, :].rearrange("p (u y) -> p u y", u=2),
+                    in0=live["scores", s, i][:].rearrange("p (u y) -> p u y", u=2),
+                    scalar=SCORE_SCALE,
+                    in1=live["dyn_rows", s][:, i, :].rearrange("p (y u) -> p u y", u=2),
+                    op0=ALU.mult,
+                    op1=ALU.mult,
+                )
+            neg_max = work.tile([P, NODE_TILES], F32)
+            nc.vector.tensor_reduce(out=neg_max[:], in_=gated[:], axis=AX.X, op=ALU.max, negate=True)
+            live["gated", s], live["neg_max", s] = gated, neg_max
+
+        def soften(s):
+            e_rows = work.tile([P, NODE_TILES, NODES], BF16)
+            row_sum = work.tile([P, NODE_TILES], F32, bufs=3)
+            for i in range(NODE_TILES):
+                nc.scalar.activation(
+                    out=e_rows[:, i, :],
+                    in_=live["gated", s][:, i, :],
+                    func=ACT.Exp,
+                    bias=live["neg_max", s][:, i : i + 1],
+                    scale=1.0,
+                    accum_out=row_sum[:, i : i + 1],
+                )
+            live["e_rows", s], live["row_sum", s] = e_rows, row_sum
+
+        def flip_e(s):
+            e_words = live["e_rows", s][:].bitcast(F32)
+            e_grouped = work.tile([P, NODE_TILES, P, PACK], BF16, align_bytes=64, bufs=3)
+            for b in range(NODE_TILES // 2):
+                e_flipped = psum.tile([P, 2, 2, P], F32, tag="e_flip", bufs=2)
+                for c in range(2):
+                    for u in range(2):
+                        nc.tensor.transpose(
+                            out=e_flipped[:, c, u, :],
+                            in_=e_words[:, 2 * b + c, u * P : (u + 1) * P],
+                            identity=ident_f32[:],
+                        )
+                nc.scalar.copy(
+                    out=e_grouped[:, 2 * b : 2 * b + 2].bitcast(F32),
+                    in_=e_flipped[:].rearrange("p c u r -> p c r u"),
+                )
+            live["e_grouped", s] = e_grouped
+
+        def pack_e(s):
+            inv_sum = work.tile([P, NODE_TILES], F32)
+            nc.vector.reciprocal(out=inv_sum[:], in_=live["row_sum", s][:])
+            e_codes = work.tile([P, NODE_TILES, P], U32, align_bytes=64)
+            e_scales = work.tile([P, NODE_TILES, P], U8, align_bytes=64)
+            nc.vector.quantize_mx(
+                out=e_codes[:].rearrange("p i r -> p (i r)").bitcast(FP8X4),
+                scales=e_scales[:].rearrange("p i r -> p (i r)"),
+                in_=live["e_grouped", s][:].rearrange("p i r j -> p (i r j)"),
+            )
+            live["inv_sum", s], live["e_codes", s], live["e_scales", s] = inv_sum, e_codes, e_scales
+
+        def attend(s):
+            t, h = s // HEADS, s % HEADS
+            o_sums = psum.tile([P, NODE_TILES, HEAD_DIM], F32, tag="sums")
+            for i in range(NODE_TILES):
+                nc.tensor.matmul_mx(
+                    out=o_sums[:, i, :],
+                    lhsT=live["e_codes", s][:, i, :].bitcast(FP8X4),
+                    lhsT_scale=live["e_scales", s][:, i, :],
+                    rhs=v_codes[:, t, h, :].bitcast(FP8X4),
+                    rhs_scale=v_scales[:, t, h, :],
+                    start=True,
+                    stop=True,
+                )
+            live["o_sums", s] = o_sums
+
+        def finish(s):
+            t, h = s // HEADS, s % HEADS
+            squashed = work.tile([P, NODE_TILES, HEAD_DIM], F32)
+            for i in range(NODE_TILES):
+                nc.scalar.activation(
+                    out=squashed[:, i, :],
+                    in_=live["o_sums", s][:, i, :],
+                    func=ACT.Tanh,
+                    scale=live["inv_sum", s][:, i : i + 1],
+                )
+            result = work.tile([P, NODE_TILES, HEAD_DIM], F32, bufs=3)
+            nc.gpsimd.tensor_tensor(out=result[:], in0=squashed[:], in1=live["h_rows", s][:], op=ALU.add)
+            nc.gpsimd.tensor_scalar(
+                out=result[:], in0=result[:], scalar1=0.5, scalar2=0.0, op0=ALU.mult, op1=ALU.add
+            )
+            nc.gpsimd.dma_start(
+                out=out[0, t].rearrange("(p i) f -> p i f", i=NODE_TILES)[:, :, h * HEAD_DIM : (h + 1) * HEAD_DIM],
+                in_=result[:],
+            )
+
+        def run(stage, s):
+            if 0 <= s < SLICES:
+                stage(s)
+
+        load_qk(0)
+        load_gate(0)
+        load_qk(1)
+        load_gate(1)
+        load_projection_operands()
+        load_qk(2)
+        load_gate(2)
+        flip_qk(0)
+        keep_qk(0)
+        score(0)
+        load_qk(3)
+        flip_qk(1)
+        keep_qk(1)
+        load_qk(4)
+        flip_qk(2)
+        keep_qk(2)
+        for s in range(SLICES + 2):
+            run(load_qk, s + 5)
+            run(load_gate, s + 3)
+            run(gate, s)
+            if s == 1:
+                project_values()
+            run(score, s + 1)
+            if s == 0:
+                flip_projection_operands()
+            run(flip_qk, s + 3)
+            run(pack_e, s - 2)
+            run(attend, s - 2)
+            run(soften, s)
+            run(finish, s - 2)
+            run(flip_e, s)
+            run(keep_qk, s + 3)

@@ -49,25 +49,22 @@ def tile_gatedspatialattentionlayer_pb_t_kernel(
 
         live = {}
 
-        w_rows = const.tile([P, HEADS, FEATURES], BF16)
-        w_grouped = const.tile([P, HEADS, FEATURE_PASSES, P, PACK], BF16, align_bytes=64)
         w_codes = const.tile([P, HEADS, FEATURE_PASSES, P], U32, align_bytes=64)
         w_scales = const.tile([P, HEADS, FEATURE_PASSES, P], U8, align_bytes=64)
         bias_rows = const.tile([P, FEATURES], BF16)
-        v_codes = const.tile([P, STEPS, HEADS, HEAD_DIM], U32, align_bytes=64)
-        v_scales = const.tile([P, STEPS, HEADS, HEAD_DIM], U8, align_bytes=64)
-        half = HEADS // 2
 
-        def load_projection_operands():
-            w_view = Wv.rearrange("(h r) f -> r h f", r=P)
-            for c in range(2):
-                heads = slice(c * half, (c + 1) * half)
-                nc.sync.dma_start(out=w_rows[:, heads, :], in_=w_view[:, heads, :])
+        def load_w(h):
+            w_rows = project.tile([P, FEATURES], BF16, bufs=3)
+            nc.sync.dma_start(out=w_rows[:], in_=Wv[h * P : (h + 1) * P, :])
+            live["w_rows", h] = w_rows
+
+        def load_bias():
             nc.sync.dma_start(out=bias_rows[:], in_=bv.partition_broadcast(P))
-            for t in range(STEPS):
-                x_rows = project.tile([P, NODE_TILES, FEATURES], BF16)
-                nc.sync.dma_start(out=x_rows[:], in_=value[0, t].rearrange("(p x) f -> p x f", x=NODE_TILES))
-                live["x_rows", t] = x_rows
+
+        def load_x(t):
+            x_rows = project.tile([P, NODE_TILES, FEATURES], BF16, bufs=2)
+            nc.sync.dma_start(out=x_rows[:], in_=value[0, t].rearrange("(p x) f -> p x f", x=NODE_TILES))
+            live["x_rows", t] = x_rows
 
         def features_to_partitions(rows, grouped):
             words = rows.bitcast(F32)
@@ -80,64 +77,72 @@ def tile_gatedspatialattentionlayer_pb_t_kernel(
                     )
             nc.scalar.copy(out=grouped.bitcast(F32), in_=flipped[:].rearrange("p g u r -> p g r u"))
 
-        def flip_projection_operands():
-            for h in range(HEADS):
-                features_to_partitions(w_rows[:, h, :], w_grouped[:, h])
-            for t in range(STEPS):
-                x_grouped = project.tile([P, NODE_TILES, FEATURE_PASSES, P, PACK], BF16, align_bytes=64)
-                for x in range(NODE_TILES):
-                    features_to_partitions(live["x_rows", t][:, x, :], x_grouped[:, x])
-                live["x_grouped", t] = x_grouped
+        def flip_w(h):
+            w_grouped = project.tile([P, FEATURE_PASSES, P, PACK], BF16, align_bytes=64, bufs=3)
+            features_to_partitions(live["w_rows", h][:], w_grouped[:])
+            live["w_grouped", h] = w_grouped
 
-        def project_values():
-            for c in range(2):
-                heads = slice(c * half, (c + 1) * half)
-                nc.vector.quantize_mx(
-                    out=w_codes[:, heads].rearrange("p h g r -> p (h g r)").bitcast(FP8X4),
-                    scales=w_scales[:, heads].rearrange("p h g r -> p (h g r)"),
-                    in_=w_grouped[:, heads].rearrange("p h g r j -> p (h g r j)"),
-                )
-            for t in range(STEPS):
-                x_codes = project.tile([P, NODE_TILES, FEATURE_PASSES, P], U32, align_bytes=64)
-                x_scales = project.tile([P, NODE_TILES, FEATURE_PASSES, P], U8, align_bytes=64)
-                nc.vector.quantize_mx(
-                    out=x_codes[:].rearrange("p x g r -> p (x g r)").bitcast(FP8X4),
-                    scales=x_scales[:].rearrange("p x g r -> p (x g r)"),
-                    in_=live["x_grouped", t][:].rearrange("p x g r j -> p (x g r j)"),
-                )
-                live["x_codes", t] = x_codes
-                live["x_scales", t] = x_scales
-            for t in range(STEPS):
-                x_codes = live["x_codes", t]
-                x_scales = live["x_scales", t]
-                v_grouped = project.tile([P, HEADS, HEAD_DIM, PACK], BF16, align_bytes=64, bufs=2)
-                for h in range(HEADS):
-                    v_sums = psum.tile([P, PACK, HEAD_DIM], F32, tag="scores", bufs=NODE_TILES)
-                    for x in range(NODE_TILES):
-                        place = 2 * (x % 2) + x // 2
-                        for g in range(FEATURE_PASSES):
-                            nc.tensor.matmul_mx(
-                                out=v_sums[:, place, :],
-                                lhsT=x_codes[:, x, g, :].bitcast(FP8X4),
-                                lhsT_scale=x_scales[:, x, g, :],
-                                rhs=w_codes[:, h, g, :].bitcast(FP8X4),
-                                rhs_scale=w_scales[:, h, g, :],
-                                start=(g == 0),
-                                stop=(g == FEATURE_PASSES - 1),
-                            )
-                    nc.vector.tensor_tensor(
-                        out=v_grouped[:, h],
-                        in0=v_sums[:].rearrange("p j d -> p d j"),
-                        in1=bias_rows[:, h * HEAD_DIM : (h + 1) * HEAD_DIM]
-                        .unsqueeze(2)
-                        .to_broadcast([P, HEAD_DIM, PACK]),
-                        op=ALU.add,
+        def pack_w(h):
+            nc.vector.quantize_mx(
+                out=w_codes[:, h].rearrange("p g r -> p (g r)").bitcast(FP8X4),
+                scales=w_scales[:, h].rearrange("p g r -> p (g r)"),
+                in_=live["w_grouped", h][:].rearrange("p g r j -> p (g r j)"),
+            )
+
+        def flip_x(t, x):
+            x_grouped = project.tile([P, FEATURE_PASSES, P, PACK], BF16, align_bytes=64, bufs=4)
+            features_to_partitions(live["x_rows", t][:, x, :], x_grouped[:])
+            live["x_grouped", t, x] = x_grouped
+
+        def pack_x(t, x):
+            x_codes = project.tile([P, FEATURE_PASSES, P], U32, align_bytes=64, bufs=2 * NODE_TILES)
+            x_scales = project.tile([P, FEATURE_PASSES, P], U8, align_bytes=64, bufs=2 * NODE_TILES)
+            nc.vector.quantize_mx(
+                out=x_codes[:].rearrange("p g r -> p (g r)").bitcast(FP8X4),
+                scales=x_scales[:].rearrange("p g r -> p (g r)"),
+                in_=live["x_grouped", t, x][:].rearrange("p g r j -> p (g r j)"),
+            )
+            live["x_codes", t, x], live["x_scales", t, x] = x_codes, x_scales
+
+        def project_v(s):
+            t, h = s // HEADS, s % HEADS
+            v_sums = psum.tile([P, PACK, HEAD_DIM], F32, tag="scores", bufs=NODE_TILES)
+            for x in range(NODE_TILES):
+                place = 2 * (x % 2) + x // 2
+                for g in range(FEATURE_PASSES):
+                    nc.tensor.matmul_mx(
+                        out=v_sums[:, place, :],
+                        lhsT=live["x_codes", t, x][:, g, :].bitcast(FP8X4),
+                        lhsT_scale=live["x_scales", t, x][:, g, :],
+                        rhs=w_codes[:, h, g, :].bitcast(FP8X4),
+                        rhs_scale=w_scales[:, h, g, :],
+                        start=(g == 0),
+                        stop=(g == FEATURE_PASSES - 1),
                     )
-                nc.vector.quantize_mx(
-                    out=v_codes[:, t].rearrange("p h d -> p (h d)").bitcast(FP8X4),
-                    scales=v_scales[:, t].rearrange("p h d -> p (h d)"),
-                    in_=v_grouped[:].rearrange("p h d j -> p (h d j)"),
-                )
+            live["v_sums", s] = v_sums
+
+        def bias_v(s):
+            h = s % HEADS
+            v_grouped = project.tile([P, HEAD_DIM, PACK], BF16, align_bytes=64, bufs=2)
+            nc.vector.tensor_tensor(
+                out=v_grouped[:],
+                in0=live["v_sums", s][:].rearrange("p j d -> p d j"),
+                in1=bias_rows[:, h * HEAD_DIM : (h + 1) * HEAD_DIM]
+                .unsqueeze(2)
+                .to_broadcast([P, HEAD_DIM, PACK]),
+                op=ALU.add,
+            )
+            live["v_grouped", s] = v_grouped
+
+        def pack_v(s):
+            v_codes = project.tile([P, HEAD_DIM], U32, align_bytes=64, bufs=4)
+            v_scales = project.tile([P, HEAD_DIM], U8, align_bytes=64, bufs=4)
+            nc.vector.quantize_mx(
+                out=v_codes[:].bitcast(FP8X4),
+                scales=v_scales[:],
+                in_=live["v_grouped", s][:].rearrange("p d j -> p (d j)"),
+            )
+            live["v_codes", s], live["v_scales", s] = v_codes, v_scales
 
         def load_qk(s):
             t, h = s // HEADS, s % HEADS
@@ -151,7 +156,7 @@ def tile_gatedspatialattentionlayer_pb_t_kernel(
             t, h = s // HEADS, s % HEADS
             dyn_rows = loads.tile([P, NODE_TILES, NODES], BF16, bufs=4)
             nc.sync.dma_start(out=dyn_rows[:], in_=dyn[h, t].rearrange("(p i) m -> p i m", i=NODE_TILES))
-            h_rows = loads.tile([P, NODE_TILES, HEAD_DIM], BF16, bufs=6)
+            h_rows = loads.tile([P, NODE_TILES, HEAD_DIM], BF16, bufs=8)
             nc.sync.dma_start(
                 out=h_rows[:],
                 in_=h_gcn[0, t].rearrange("(p i) f -> p i f", i=NODE_TILES)[:, :, h * HEAD_DIM : (h + 1) * HEAD_DIM],
@@ -200,13 +205,16 @@ def tile_gatedspatialattentionlayer_pb_t_kernel(
                     op0=ALU.mult,
                     op1=ALU.mult,
                 )
+            live["gated", s] = gated
+
+        def top(s):
             neg_max = work.tile([P, NODE_TILES], F32)
-            nc.vector.tensor_reduce(out=neg_max[:], in_=gated[:], axis=AX.X, op=ALU.max, negate=True)
-            live["gated", s], live["neg_max", s] = gated, neg_max
+            nc.vector.tensor_reduce(out=neg_max[:], in_=live["gated", s][:], axis=AX.X, op=ALU.max, negate=True)
+            live["neg_max", s] = neg_max
 
         def soften(s):
             e_rows = work.tile([P, NODE_TILES, NODES], BF16)
-            row_sum = work.tile([P, NODE_TILES], F32, bufs=3)
+            row_sum = work.tile([P, NODE_TILES], F32, bufs=5)
             for i in range(NODE_TILES):
                 nc.scalar.activation(
                     out=e_rows[:, i, :],
@@ -220,7 +228,7 @@ def tile_gatedspatialattentionlayer_pb_t_kernel(
 
         def flip_e(s):
             e_words = live["e_rows", s][:].bitcast(F32)
-            e_grouped = work.tile([P, NODE_TILES, P, PACK], BF16, align_bytes=64, bufs=3)
+            e_grouped = work.tile([P, NODE_TILES, P, PACK], BF16, align_bytes=64, bufs=5)
             for b in range(NODE_TILES // 2):
                 e_flipped = psum.tile([P, 2, 2, P], F32, tag="e_flip", bufs=2)
                 for c in range(2):
@@ -249,15 +257,14 @@ def tile_gatedspatialattentionlayer_pb_t_kernel(
             live["inv_sum", s], live["e_codes", s], live["e_scales", s] = inv_sum, e_codes, e_scales
 
         def attend(s):
-            t, h = s // HEADS, s % HEADS
             o_sums = psum.tile([P, NODE_TILES, HEAD_DIM], F32, tag="sums")
             for i in range(NODE_TILES):
                 nc.tensor.matmul_mx(
                     out=o_sums[:, i, :],
                     lhsT=live["e_codes", s][:, i, :].bitcast(FP8X4),
                     lhsT_scale=live["e_scales", s][:, i, :],
-                    rhs=v_codes[:, t, h, :].bitcast(FP8X4),
-                    rhs_scale=v_scales[:, t, h, :],
+                    rhs=live["v_codes", s][:].bitcast(FP8X4),
+                    rhs_scale=live["v_scales", s][:],
                     start=True,
                     stop=True,
                 )
@@ -278,9 +285,13 @@ def tile_gatedspatialattentionlayer_pb_t_kernel(
             nc.gpsimd.tensor_scalar(
                 out=result[:], in0=result[:], scalar1=0.5, scalar2=0.0, op0=ALU.mult, op1=ALU.add
             )
-            nc.gpsimd.dma_start(
+            live["result", s] = result
+
+        def store(s):
+            t, h = s // HEADS, s % HEADS
+            nc.sync.dma_start(
                 out=out[0, t].rearrange("(p i) f -> p i f", i=NODE_TILES)[:, :, h * HEAD_DIM : (h + 1) * HEAD_DIM],
-                in_=result[:],
+                in_=live["result", s][:],
             )
 
         def run(stage, s):
@@ -289,11 +300,15 @@ def tile_gatedspatialattentionlayer_pb_t_kernel(
 
         load_qk(0)
         load_gate(0)
+        load_x(0)
+        load_w(0)
         load_qk(1)
         load_gate(1)
-        load_projection_operands()
+        load_bias()
+        load_w(1)
         load_qk(2)
         load_gate(2)
+        load_w(2)
         flip_qk(0)
         keep_qk(0)
         score(0)
@@ -303,19 +318,39 @@ def tile_gatedspatialattentionlayer_pb_t_kernel(
         load_qk(4)
         flip_qk(2)
         keep_qk(2)
-        for s in range(SLICES + 2):
+        for s in range(SLICES + 4):
+            run(store, s - 4)
             run(load_qk, s + 5)
             run(load_gate, s + 3)
+            if s + 3 < HEADS:
+                load_w(s + 3)
+            if s % HEADS == 1 and s // HEADS + 1 < STEPS:
+                load_x(s // HEADS + 1)
+            later, part = (s + 4) // HEADS, (s + 4) % HEADS - 1
             run(gate, s)
-            if s == 1:
-                project_values()
+            run(project_v, s - 2)
+            run(bias_v, s - 2)
             run(score, s + 1)
-            if s == 0:
-                flip_projection_operands()
+            run(top, s)
+            if s == 1:
+                for x in range(NODE_TILES):
+                    pack_x(0, x)
+            if 1 <= s <= HEADS:
+                pack_w(s - 1)
+            if 1 <= later < STEPS and 0 <= part < NODE_TILES:
+                pack_x(later, part)
+            run(soften, s - 1)
+            run(attend, s - 3)
+            run(finish, s - 3)
+            run(flip_e, s - 1)
             run(flip_qk, s + 3)
-            run(pack_e, s - 2)
-            run(attend, s - 2)
-            run(soften, s)
-            run(finish, s - 2)
-            run(flip_e, s)
             run(keep_qk, s + 3)
+            if s == 0:
+                for x in range(NODE_TILES):
+                    flip_x(0, x)
+            if s < HEADS:
+                flip_w(s)
+            if 1 <= later < STEPS and 0 <= part + 1 < NODE_TILES:
+                flip_x(later, part + 1)
+            run(pack_v, s - 2)
+            run(pack_e, s - 2)

@@ -245,10 +245,10 @@ def tile_gatedspatialattentionlayer_pb_t_kernel(
             live["e_grouped", s] = e_grouped
 
         def pack_e(s):
-            inv_sum = work.tile([P, NODE_TILES], F32)
+            inv_sum = work.tile([P, NODE_TILES], F32, bufs=4)
             nc.vector.reciprocal(out=inv_sum[:], in_=live["row_sum", s][:])
-            e_codes = work.tile([P, NODE_TILES, P], U32, align_bytes=64)
-            e_scales = work.tile([P, NODE_TILES, P], U8, align_bytes=64)
+            e_codes = work.tile([P, NODE_TILES, P], U32, align_bytes=64, bufs=4)
+            e_scales = work.tile([P, NODE_TILES, P], U8, align_bytes=64, bufs=4)
             nc.vector.quantize_mx(
                 out=e_codes[:].rearrange("p i r -> p (i r)").bitcast(FP8X4),
                 scales=e_scales[:].rearrange("p i r -> p (i r)"),
@@ -300,15 +300,14 @@ def tile_gatedspatialattentionlayer_pb_t_kernel(
 
         load_qk(0)
         load_gate(0)
-        load_x(0)
-        load_w(0)
         load_qk(1)
         load_gate(1)
-        load_bias()
-        load_w(1)
+        load_x(0)
+        load_w(0)
         load_qk(2)
         load_gate(2)
-        load_w(2)
+        load_bias()
+        load_w(1)
         flip_qk(0)
         keep_qk(0)
         score(0)
@@ -316,41 +315,47 @@ def tile_gatedspatialattentionlayer_pb_t_kernel(
         flip_qk(1)
         keep_qk(1)
         load_qk(4)
-        flip_qk(2)
-        keep_qk(2)
         for s in range(SLICES + 4):
-            run(store, s - 4)
+            run(store, s - 5)
             run(load_qk, s + 5)
             run(load_gate, s + 3)
-            if s + 3 < HEADS:
-                load_w(s + 3)
+            if s + 2 < HEADS:
+                load_w(s + 2)
             if s % HEADS == 1 and s // HEADS + 1 < STEPS:
                 load_x(s // HEADS + 1)
-            later, part = (s + 4) // HEADS, (s + 4) % HEADS - 1
+            done = [j for j in range(SLICES) if max(j + STEPS - j // HEADS, j + 2) + 1 == s]
+            for j in done:
+                run(attend, j)
             run(gate, s)
-            run(project_v, s - 2)
-            run(bias_v, s - 2)
+            values = [j for j in range(SLICES) if j + STEPS - j // HEADS == s]
+            for j in values:
+                run(project_v, j)
+                run(bias_v, j)
             run(score, s + 1)
             run(top, s)
-            if s == 1:
-                for x in range(NODE_TILES):
+            if 1 <= s <= 2:
+                for x in range(2 * s - 2, 2 * s):
                     pack_x(0, x)
-            if 1 <= s <= HEADS:
-                pack_w(s - 1)
+            if 2 <= s < HEADS + 2:
+                pack_w(s - 2)
+            later, part = (s + 4) // HEADS, (s + 4) % HEADS - 1
             if 1 <= later < STEPS and 0 <= part < NODE_TILES:
                 pack_x(later, part)
             run(soften, s - 1)
-            run(attend, s - 3)
-            run(finish, s - 3)
+            for j in done:
+                run(finish, j)
             run(flip_e, s - 1)
-            run(flip_qk, s + 3)
-            run(keep_qk, s + 3)
-            if s == 0:
-                for x in range(NODE_TILES):
+            run(flip_qk, s + 2)
+            run(keep_qk, s + 2)
+            if s < 2:
+                for x in range(2 * s, 2 * s + 2):
                     flip_x(0, x)
-            if s < HEADS:
-                flip_w(s)
+            if 1 <= s < HEADS + 1:
+                flip_w(s - 1)
             if 1 <= later < STEPS and 0 <= part + 1 < NODE_TILES:
                 flip_x(later, part + 1)
-            run(pack_v, s - 2)
+            for j in values:
+                run(pack_v, j)
             run(pack_e, s - 2)
+        for s in range(SLICES - 1, SLICES):
+            store(s)

@@ -28,6 +28,7 @@ FLOPS = 2 * STEPS * NODES * FEATURES * FEATURES + 2 * (2 * STEPS * HEADS * NODES
 
 
 SLICES = STEPS * HEADS
+LAST = SLICES - 1
 
 
 def tile_gatedspatialattentionlayer_pb_t_kernel(
@@ -61,10 +62,10 @@ def tile_gatedspatialattentionlayer_pb_t_kernel(
         def load_bias():
             nc.sync.dma_start(out=bias_rows[:], in_=bv.partition_broadcast(P))
 
-        def load_x(t):
-            x_rows = project.tile([P, NODE_TILES, FEATURES], BF16, bufs=2)
-            nc.sync.dma_start(out=x_rows[:], in_=value[0, t].rearrange("(p x) f -> p x f", x=NODE_TILES))
-            live["x_rows", t] = x_rows
+        def load_x(t, x):
+            x_rows = project.tile([P, FEATURES], BF16, bufs=4)
+            nc.sync.dma_start(out=x_rows[:], in_=value[0, t].rearrange("(p x) f -> p x f", x=NODE_TILES)[:, x, :])
+            live["x_rows", t, x] = x_rows
 
         def features_to_partitions(rows, grouped):
             words = rows.bitcast(F32)
@@ -91,7 +92,7 @@ def tile_gatedspatialattentionlayer_pb_t_kernel(
 
         def flip_x(t, x):
             x_grouped = project.tile([P, FEATURE_PASSES, P, PACK], BF16, align_bytes=64, bufs=4)
-            features_to_partitions(live["x_rows", t][:, x, :], x_grouped[:])
+            features_to_partitions(live["x_rows", t, x][:], x_grouped[:])
             live["x_grouped", t, x] = x_grouped
 
         def pack_x(t, x):
@@ -134,6 +135,21 @@ def tile_gatedspatialattentionlayer_pb_t_kernel(
             )
             live["v_grouped", s] = v_grouped
 
+        def bias_v_beside(s):
+            h = s % HEADS
+            v_plain = project.tile([P, HEAD_DIM, PACK], F32, bufs=2)
+            nc.scalar.copy(out=v_plain[:], in_=live["v_sums", s][:].rearrange("p j d -> p d j"))
+            v_grouped = project.tile([P, HEAD_DIM, PACK], BF16, align_bytes=64, bufs=2)
+            nc.gpsimd.tensor_tensor(
+                out=v_grouped[:],
+                in0=v_plain[:],
+                in1=bias_rows[:, h * HEAD_DIM : (h + 1) * HEAD_DIM]
+                .unsqueeze(2)
+                .to_broadcast([P, HEAD_DIM, PACK]),
+                op=ALU.add,
+            )
+            live["v_grouped", s] = v_grouped
+
         def pack_v(s):
             v_codes = project.tile([P, HEAD_DIM], U32, align_bytes=64, bufs=4)
             v_scales = project.tile([P, HEAD_DIM], U8, align_bytes=64, bufs=4)
@@ -156,12 +172,16 @@ def tile_gatedspatialattentionlayer_pb_t_kernel(
             t, h = s // HEADS, s % HEADS
             dyn_rows = loads.tile([P, NODE_TILES, NODES], BF16, bufs=4)
             nc.sync.dma_start(out=dyn_rows[:], in_=dyn[h, t].rearrange("(p i) m -> p i m", i=NODE_TILES))
+            live["dyn_rows", s] = dyn_rows
+
+        def load_h(s):
+            t, h = s // HEADS, s % HEADS
             h_rows = loads.tile([P, NODE_TILES, HEAD_DIM], BF16, bufs=8)
             nc.sync.dma_start(
                 out=h_rows[:],
                 in_=h_gcn[0, t].rearrange("(p i) f -> p i f", i=NODE_TILES)[:, :, h * HEAD_DIM : (h + 1) * HEAD_DIM],
             )
-            live["dyn_rows", s], live["h_rows", s] = dyn_rows, h_rows
+            live["h_rows", s] = h_rows
 
         def flip_qk(s):
             qk_flipped = psum.tile([P, 2 * NODE_TILES, P], BF16, tag="flip")
@@ -197,20 +217,35 @@ def tile_gatedspatialattentionlayer_pb_t_kernel(
         def gate(s):
             gated = work.tile([P, NODE_TILES, NODES], F32)
             for i in range(NODE_TILES):
-                nc.vector.scalar_tensor_tensor(
-                    out=gated[:, i, :].rearrange("p (u y) -> p u y", u=2),
-                    in0=live["scores", s, i][:].rearrange("p (u y) -> p u y", u=2),
-                    scalar=SCORE_SCALE,
-                    in1=live["dyn_rows", s][:, i, :].rearrange("p (y u) -> p u y", u=2),
-                    op0=ALU.mult,
-                    op1=ALU.mult,
-                )
+                gate_tile(s, i, gated)
             live["gated", s] = gated
 
         def top(s):
             neg_max = work.tile([P, NODE_TILES], F32)
             nc.vector.tensor_reduce(out=neg_max[:], in_=live["gated", s][:], axis=AX.X, op=ALU.max, negate=True)
             live["neg_max", s] = neg_max
+
+        def gate_tile(s, i, gated):
+            nc.vector.scalar_tensor_tensor(
+                out=gated[:, i, :].rearrange("p (u y) -> p u y", u=2),
+                in0=live["scores", s, i][:].rearrange("p (u y) -> p u y", u=2),
+                scalar=SCORE_SCALE,
+                in1=live["dyn_rows", s][:, i, :].rearrange("p (y u) -> p u y", u=2),
+                op0=ALU.mult,
+                op1=ALU.mult,
+            )
+
+        def gate_last(s):
+            gated = work.tile([P, NODE_TILES, NODES], F32)
+            neg_max = work.tile([P, NODE_TILES], F32)
+            for i in range(NODE_TILES + 1):
+                if i < NODE_TILES:
+                    gate_tile(s, i, gated)
+                if i > 0:
+                    nc.vector.tensor_reduce(
+                        out=neg_max[:, i - 1 : i], in_=gated[:, i - 1, :], axis=AX.X, op=ALU.max, negate=True
+                    )
+            live["gated", s], live["neg_max", s] = gated, neg_max
 
         def soften(s):
             e_rows = work.tile([P, NODE_TILES, NODES], BF16)
@@ -238,22 +273,26 @@ def tile_gatedspatialattentionlayer_pb_t_kernel(
                             in_=e_words[:, 2 * b + c, u * P : (u + 1) * P],
                             identity=ident_f32[:],
                         )
-                nc.scalar.copy(
+                copy = nc.vector.tensor_copy if s == LAST and b == 1 else nc.scalar.copy
+                copy(
                     out=e_grouped[:, 2 * b : 2 * b + 2].bitcast(F32),
                     in_=e_flipped[:].rearrange("p c u r -> p c r u"),
                 )
             live["e_grouped", s] = e_grouped
 
         def pack_e(s):
-            inv_sum = work.tile([P, NODE_TILES], F32, bufs=4)
+            inv_sum = work.tile([P, NODE_TILES], F32, bufs=5)
             nc.vector.reciprocal(out=inv_sum[:], in_=live["row_sum", s][:])
-            e_codes = work.tile([P, NODE_TILES, P], U32, align_bytes=64, bufs=4)
-            e_scales = work.tile([P, NODE_TILES, P], U8, align_bytes=64, bufs=4)
-            nc.vector.quantize_mx(
-                out=e_codes[:].rearrange("p i r -> p (i r)").bitcast(FP8X4),
-                scales=e_scales[:].rearrange("p i r -> p (i r)"),
-                in_=live["e_grouped", s][:].rearrange("p i r j -> p (i r j)"),
-            )
+            e_codes = work.tile([P, NODE_TILES, P], U32, align_bytes=64, bufs=5)
+            e_scales = work.tile([P, NODE_TILES, P], U8, align_bytes=64, bufs=5)
+            width = NODE_TILES // 2 if s == LAST else NODE_TILES
+            for i in range(0, NODE_TILES, width):
+                tiles = slice(i, i + width)
+                nc.vector.quantize_mx(
+                    out=e_codes[:, tiles].rearrange("p i r -> p (i r)").bitcast(FP8X4),
+                    scales=e_scales[:, tiles].rearrange("p i r -> p (i r)"),
+                    in_=live["e_grouped", s][:, tiles].rearrange("p i r j -> p (i r j)"),
+                )
             live["inv_sum", s], live["e_codes", s], live["e_scales", s] = inv_sum, e_codes, e_scales
 
         def attend(s):
@@ -287,6 +326,41 @@ def tile_gatedspatialattentionlayer_pb_t_kernel(
             )
             live["result", s] = result
 
+        def halve_h(s):
+            h_half = work.tile([P, NODE_TILES, HEAD_DIM], F32)
+            nc.gpsimd.tensor_scalar(
+                out=h_half[:], in0=live["h_rows", s][:], scalar1=0.5, scalar2=0.0, op0=ALU.mult, op1=ALU.add
+            )
+            live["h_half", s] = h_half
+
+        def finish_last(s):
+            t, h = s // HEADS, s % HEADS
+            squashed = work.tile([P, NODE_TILES, HEAD_DIM], F32)
+            result = work.tile([P, NODE_TILES, HEAD_DIM], F32, bufs=3)
+            for b in range(2):
+                tiles = slice(2 * b, 2 * b + 2)
+                for i in range(2 * b, 2 * b + 2):
+                    nc.scalar.activation(
+                        out=squashed[:, i, :],
+                        in_=live["o_sums", s][:, i, :],
+                        func=ACT.Tanh,
+                        scale=live["inv_sum", s][:, i : i + 1],
+                    )
+                nc.vector.scalar_tensor_tensor(
+                    out=result[:, tiles, :],
+                    in0=squashed[:, tiles, :],
+                    scalar=0.5,
+                    in1=live["h_half", s][:, tiles, :],
+                    op0=ALU.mult,
+                    op1=ALU.add,
+                )
+                nc.sync.dma_start(
+                    out=out[0, t].rearrange("(p i) f -> p i f", i=NODE_TILES)[
+                        :, tiles, h * HEAD_DIM : (h + 1) * HEAD_DIM
+                    ],
+                    in_=result[:, tiles, :],
+                )
+
         def store(s):
             t, h = s // HEADS, s % HEADS
             nc.sync.dma_start(
@@ -298,11 +372,23 @@ def tile_gatedspatialattentionlayer_pb_t_kernel(
             if 0 <= s < SLICES:
                 stage(s)
 
+        def pack(s):
+            for j in range(SLICES):
+                if j + lag(j) + 1 == s:
+                    pack_v(j)
+            run(pack_e, s - 2)
+
+        def lag(j):
+            return 3 - j // 6
+
         load_qk(0)
         load_gate(0)
         load_qk(1)
+        load_x(0, 0)
+        load_x(0, 1)
         load_gate(1)
-        load_x(0)
+        load_x(0, 2)
+        load_x(0, 3)
         load_w(0)
         load_qk(2)
         load_gate(2)
@@ -311,51 +397,68 @@ def tile_gatedspatialattentionlayer_pb_t_kernel(
         flip_qk(0)
         keep_qk(0)
         score(0)
-        load_qk(3)
         flip_qk(1)
         keep_qk(1)
-        load_qk(4)
-        for s in range(SLICES + 4):
-            run(store, s - 5)
-            run(load_qk, s + 5)
+        for s in range(SLICES + 3):
+            for j in range(LAST - 1):
+                if j + max(lag(j) + 2, 3) == s - 1:
+                    store(j)
+            run(load_qk, s + 3)
             run(load_gate, s + 3)
             if s + 2 < HEADS:
                 load_w(s + 2)
-            if s % HEADS == 1 and s // HEADS + 1 < STEPS:
-                load_x(s // HEADS + 1)
-            done = [j for j in range(SLICES) if max(j + STEPS - j // HEADS, j + 2) + 1 == s]
+            run(load_h, s - 0)
+            ahead, part = (s + 6) // HEADS, (s + 6) % HEADS
+            if 1 <= ahead < STEPS and part < NODE_TILES:
+                load_x(ahead, part)
+            values = [j for j in range(SLICES) if j + lag(j) == s]
+            done = [j for j in range(SLICES) if j + max(lag(j) + 2, 3) == s]
             for j in done:
-                run(attend, j)
-            run(gate, s)
-            values = [j for j in range(SLICES) if j + STEPS - j // HEADS == s]
+                attend(j)
+            if s >= LAST:
+                pack(s)
+            if s == LAST:
+                gate_last(s)
+                halve_h(s - 1)
+                halve_h(s)
+            else:
+                run(gate, s)
             for j in values:
-                run(project_v, j)
-                run(bias_v, j)
+                project_v(j)
+                if not (j % 2 == 1 and j < SLICES - 3):
+                    bias_v(j)
             run(score, s + 1)
-            run(top, s)
+            if s != LAST:
+                run(top, s)
             if 1 <= s <= 2:
                 for x in range(2 * s - 2, 2 * s):
                     pack_x(0, x)
-            if 2 <= s < HEADS + 2:
-                pack_w(s - 2)
+            if 1 <= s < HEADS + 1:
+                pack_w(s - 1)
             later, part = (s + 4) // HEADS, (s + 4) % HEADS - 1
             if 1 <= later < STEPS and 0 <= part < NODE_TILES:
                 pack_x(later, part)
-            run(soften, s - 1)
+            if s != LAST + 1:
+                run(soften, s - 1)
+            for j in values:
+                if j % 2 == 1 and j < SLICES - 3:
+                    bias_v_beside(j)
             for j in done:
-                run(finish, j)
+                if j >= LAST - 1:
+                    finish_last(j)
+                else:
+                    finish(j)
+            if s == LAST + 1:
+                soften(LAST)
             run(flip_e, s - 1)
             run(flip_qk, s + 2)
             run(keep_qk, s + 2)
             if s < 2:
                 for x in range(2 * s, 2 * s + 2):
                     flip_x(0, x)
-            if 1 <= s < HEADS + 1:
-                flip_w(s - 1)
+            if s < HEADS:
+                flip_w(s)
             if 1 <= later < STEPS and 0 <= part + 1 < NODE_TILES:
                 flip_x(later, part + 1)
-            for j in values:
-                run(pack_v, j)
-            run(pack_e, s - 2)
-        for s in range(SLICES - 1, SLICES):
-            store(s)
+            if s < LAST:
+                pack(s)

@@ -438,16 +438,17 @@ def tile_gatedspatialattentionlayer_pb_t_kernel(
             later, part = (s + 4) // HEADS, (s + 4) % HEADS - 1
             if 1 <= later < STEPS and 0 <= part < NODE_TILES:
                 pack_x(later, part)
-            if s != LAST + 1:
-                run(soften, s - 1)
+            if s > LAST + 1:
+                for j in done:
+                    finish_last(j)
+            else:
+                for j in done:
+                    finish(j)
             for j in values:
                 if j % 2 == 1 and j < SLICES - 3:
                     bias_v_beside(j)
-            for j in done:
-                if j >= LAST - 1:
-                    finish_last(j)
-                else:
-                    finish(j)
+            if s != LAST + 1:
+                run(soften, s - 1)
             if s == LAST + 1:
                 soften(LAST)
             run(flip_e, s - 1)

@@ -26,7 +26,6 @@ SCORE_SCALE = 1.0 / math.sqrt(HEAD_DIM)
 
 FLOPS = 2 * STEPS * NODES * FEATURES * FEATURES + 2 * (2 * STEPS * HEADS * NODES * NODES * HEAD_DIM)
 
-
 SLICES = STEPS * HEADS
 LAST = SLICES - 1
 
@@ -38,7 +37,7 @@ def tile_gatedspatialattentionlayer_pb_t_kernel(
     with ExitStack() as ctx:
         ctx.enter_context(tc.manual_schedule())
         const = ctx.enter_context(tc.tile_pool(name="const", bufs=1))
-        project = ctx.enter_context(tc.tile_pool(name="project", bufs=STEPS))
+        project = ctx.enter_context(tc.tile_pool(name="project", bufs=2))
         loads = ctx.enter_context(tc.tile_pool(name="loads", bufs=3))
         work = ctx.enter_context(tc.tile_pool(name="work", bufs=2))
         psum = ctx.enter_context(tc.psum_pool(name="psum", bufs=1))
@@ -47,29 +46,28 @@ def tile_gatedspatialattentionlayer_pb_t_kernel(
         make_identity(nc, ident_bf16[:])
         ident_f32 = const.tile([P, P], F32)
         make_identity(nc, ident_f32[:])
+        bias_rows = const.tile([P, FEATURES], BF16)
+        w_codes = const.tile([P, HEADS, FEATURE_PASSES, P], U32, align_bytes=64)
+        w_scales = const.tile([P, HEADS, FEATURE_PASSES, P], U8, align_bytes=64)
 
         live = {}
 
-        w_codes = const.tile([P, HEADS, FEATURE_PASSES, P], U32, align_bytes=64)
-        w_scales = const.tile([P, HEADS, FEATURE_PASSES, P], U8, align_bytes=64)
-        bias_rows = const.tile([P, FEATURES], BF16)
+        def load_bias():
+            nc.sync.dma_start(out=bias_rows[:], in_=bv.partition_broadcast(P))
 
         def load_w(h):
             w_rows = project.tile([P, FEATURES], BF16, bufs=3)
             nc.sync.dma_start(out=w_rows[:], in_=Wv[h * P : (h + 1) * P, :])
             live["w_rows", h] = w_rows
 
-        def load_bias():
-            nc.sync.dma_start(out=bias_rows[:], in_=bv.partition_broadcast(P))
-
-        def load_x(t, x):
-            x_rows = project.tile([P, FEATURES], BF16, bufs=4)
-            nc.sync.dma_start(out=x_rows[:], in_=value[0, t].rearrange("(p x) f -> p x f", x=NODE_TILES)[:, x, :])
-            live["x_rows", t, x] = x_rows
+        def load_x(t, c):
+            x_rows = project.tile([P, FEATURES], BF16, bufs=5)
+            nc.sync.dma_start(out=x_rows[:], in_=value[0, t].rearrange("(p c) f -> p c f", c=NODE_TILES)[:, c, :])
+            live["x_rows", t, c] = x_rows
 
         def features_to_partitions(rows, grouped):
             words = rows.bitcast(F32)
-            flipped = psum.tile([P, FEATURE_PASSES, 2, P], F32, tag="e_flip", bufs=2)
+            flipped = psum.tile([P, FEATURE_PASSES, 2, P], F32, tag="words", bufs=2)
             for g in range(FEATURE_PASSES):
                 for u in range(2):
                     first = (2 * g + u) * P
@@ -90,31 +88,31 @@ def tile_gatedspatialattentionlayer_pb_t_kernel(
                 in_=live["w_grouped", h][:].rearrange("p g r j -> p (g r j)"),
             )
 
-        def flip_x(t, x):
-            x_grouped = project.tile([P, FEATURE_PASSES, P, PACK], BF16, align_bytes=64, bufs=4)
-            features_to_partitions(live["x_rows", t, x][:], x_grouped[:])
-            live["x_grouped", t, x] = x_grouped
+        def flip_x(t, c):
+            x_grouped = project.tile([P, FEATURE_PASSES, P, PACK], BF16, align_bytes=64, bufs=5)
+            features_to_partitions(live["x_rows", t, c][:], x_grouped[:])
+            live["x_grouped", t, c] = x_grouped
 
-        def pack_x(t, x):
+        def pack_x(t, c):
             x_codes = project.tile([P, FEATURE_PASSES, P], U32, align_bytes=64, bufs=2 * NODE_TILES)
             x_scales = project.tile([P, FEATURE_PASSES, P], U8, align_bytes=64, bufs=2 * NODE_TILES)
             nc.vector.quantize_mx(
                 out=x_codes[:].rearrange("p g r -> p (g r)").bitcast(FP8X4),
                 scales=x_scales[:].rearrange("p g r -> p (g r)"),
-                in_=live["x_grouped", t, x][:].rearrange("p g r j -> p (g r j)"),
+                in_=live["x_grouped", t, c][:].rearrange("p g r j -> p (g r j)"),
             )
-            live["x_codes", t, x], live["x_scales", t, x] = x_codes, x_scales
+            live["x_codes", t, c], live["x_scales", t, c] = x_codes, x_scales
 
         def project_v(s):
             t, h = s // HEADS, s % HEADS
-            v_sums = psum.tile([P, PACK, HEAD_DIM], F32, tag="scores", bufs=NODE_TILES)
-            for x in range(NODE_TILES):
-                place = 2 * (x % 2) + x // 2
+            v_sums = psum.tile([P, PACK, HEAD_DIM], F32, tag="scores", bufs=4)
+            for c in range(NODE_TILES):
+                place = 2 * (c % 2) + c // 2
                 for g in range(FEATURE_PASSES):
                     nc.tensor.matmul_mx(
                         out=v_sums[:, place, :],
-                        lhsT=live["x_codes", t, x][:, g, :].bitcast(FP8X4),
-                        lhsT_scale=live["x_scales", t, x][:, g, :],
+                        lhsT=live["x_codes", t, c][:, g, :].bitcast(FP8X4),
+                        lhsT_scale=live["x_scales", t, c][:, g, :],
                         rhs=w_codes[:, h, g, :].bitcast(FP8X4),
                         rhs_scale=w_scales[:, h, g, :],
                         start=(g == 0),
@@ -122,37 +120,28 @@ def tile_gatedspatialattentionlayer_pb_t_kernel(
                     )
             live["v_sums", s] = v_sums
 
-        def bias_v(s):
+        def bias_of(s):
             h = s % HEADS
-            v_grouped = project.tile([P, HEAD_DIM, PACK], BF16, align_bytes=64, bufs=2)
+            row = bias_rows[:, h * HEAD_DIM : (h + 1) * HEAD_DIM]
+            return row.unsqueeze(2).to_broadcast([P, HEAD_DIM, PACK])
+
+        def bias_v(s):
+            v_grouped = project.tile([P, HEAD_DIM, PACK], BF16, align_bytes=64, bufs=4)
             nc.vector.tensor_tensor(
-                out=v_grouped[:],
-                in0=live["v_sums", s][:].rearrange("p j d -> p d j"),
-                in1=bias_rows[:, h * HEAD_DIM : (h + 1) * HEAD_DIM]
-                .unsqueeze(2)
-                .to_broadcast([P, HEAD_DIM, PACK]),
-                op=ALU.add,
+                out=v_grouped[:], in0=live["v_sums", s][:].rearrange("p j d -> p d j"), in1=bias_of(s), op=ALU.add
             )
             live["v_grouped", s] = v_grouped
 
         def bias_v_beside(s):
-            h = s % HEADS
-            v_plain = project.tile([P, HEAD_DIM, PACK], F32, bufs=2)
+            v_plain = project.tile([P, HEAD_DIM, PACK], F32)
             nc.scalar.copy(out=v_plain[:], in_=live["v_sums", s][:].rearrange("p j d -> p d j"))
-            v_grouped = project.tile([P, HEAD_DIM, PACK], BF16, align_bytes=64, bufs=2)
-            nc.gpsimd.tensor_tensor(
-                out=v_grouped[:],
-                in0=v_plain[:],
-                in1=bias_rows[:, h * HEAD_DIM : (h + 1) * HEAD_DIM]
-                .unsqueeze(2)
-                .to_broadcast([P, HEAD_DIM, PACK]),
-                op=ALU.add,
-            )
+            v_grouped = project.tile([P, HEAD_DIM, PACK], BF16, align_bytes=64, bufs=4)
+            nc.gpsimd.tensor_tensor(out=v_grouped[:], in0=v_plain[:], in1=bias_of(s), op=ALU.add)
             live["v_grouped", s] = v_grouped
 
         def pack_v(s):
-            v_codes = project.tile([P, HEAD_DIM], U32, align_bytes=64, bufs=4)
-            v_scales = project.tile([P, HEAD_DIM], U8, align_bytes=64, bufs=4)
+            v_codes = project.tile([P, HEAD_DIM], U32, align_bytes=64, bufs=5)
+            v_scales = project.tile([P, HEAD_DIM], U8, align_bytes=64, bufs=5)
             nc.vector.quantize_mx(
                 out=v_codes[:].bitcast(FP8X4),
                 scales=v_scales[:],
@@ -162,15 +151,15 @@ def tile_gatedspatialattentionlayer_pb_t_kernel(
 
         def load_qk(s):
             t, h = s // HEADS, s % HEADS
-            q_rows = loads.tile([P, NODE_TILES, HEAD_DIM], BF16)
+            q_rows = loads.tile([P, NODE_TILES, HEAD_DIM], BF16, bufs=5)
             nc.sync.dma_start(out=q_rows[:], in_=q_heads[h, t].rearrange("(p i) d -> p i d", i=NODE_TILES))
-            k_rows = loads.tile([P, 2, 2, HEAD_DIM], BF16)
+            k_rows = loads.tile([P, 2, 2, HEAD_DIM], BF16, bufs=5)
             nc.sync.dma_start(out=k_rows[:], in_=k_heads[h, t].rearrange("(a p u) d -> p a u d", a=2, u=2))
             live["q_rows", s], live["k_rows", s] = q_rows, k_rows
 
         def load_gate(s):
             t, h = s // HEADS, s % HEADS
-            dyn_rows = loads.tile([P, NODE_TILES, NODES], BF16, bufs=4)
+            dyn_rows = loads.tile([P, NODE_TILES, NODES], BF16, bufs=6)
             nc.sync.dma_start(out=dyn_rows[:], in_=dyn[h, t].rearrange("(p i) m -> p i m", i=NODE_TILES))
             live["dyn_rows", s] = dyn_rows
 
@@ -201,10 +190,10 @@ def tile_gatedspatialattentionlayer_pb_t_kernel(
             nc.scalar.copy(out=qk_t[:], in_=live["qk_flipped", s][:])
             live["qk_t", s] = qk_t
 
-        def score(s):
-            qk_t = live["qk_t", s]
-            for i in range(NODE_TILES):
-                scores = psum.tile([P, NODES], F32, tag="scores", bufs=NODE_TILES)
+        def score(s, i):
+            if s < SLICES:
+                qk_t = live["qk_t", s]
+                scores = psum.tile([P, NODES], F32, tag="scores", bufs=4)
                 nc.tensor.matmul(
                     out=scores[:],
                     lhsT=qk_t[:, i, :],
@@ -214,20 +203,13 @@ def tile_gatedspatialattentionlayer_pb_t_kernel(
                 )
                 live["scores", s, i] = scores
 
-        def gate(s):
-            gated = work.tile([P, NODE_TILES, NODES], F32)
-            for i in range(NODE_TILES):
-                gate_tile(s, i, gated)
-            live["gated", s] = gated
-
-        def top(s):
-            neg_max = work.tile([P, NODE_TILES], F32)
-            nc.vector.tensor_reduce(out=neg_max[:], in_=live["gated", s][:], axis=AX.X, op=ALU.max, negate=True)
-            live["neg_max", s] = neg_max
-
-        def gate_tile(s, i, gated):
+        def gate(s, i):
+            if i == 0:
+                gated = work.tile([P, NODE_TILES, NODES], F32)
+                neg_max = work.tile([P, NODE_TILES], F32)
+                live["gated", s], live["neg_max", s] = gated, neg_max
             nc.vector.scalar_tensor_tensor(
-                out=gated[:, i, :].rearrange("p (u y) -> p u y", u=2),
+                out=live["gated", s][:, i, :].rearrange("p (u y) -> p u y", u=2),
                 in0=live["scores", s, i][:].rearrange("p (u y) -> p u y", u=2),
                 scalar=SCORE_SCALE,
                 in1=live["dyn_rows", s][:, i, :].rearrange("p (y u) -> p u y", u=2),
@@ -235,17 +217,14 @@ def tile_gatedspatialattentionlayer_pb_t_kernel(
                 op1=ALU.mult,
             )
 
-        def gate_last(s):
-            gated = work.tile([P, NODE_TILES, NODES], F32)
-            neg_max = work.tile([P, NODE_TILES], F32)
-            for i in range(NODE_TILES + 1):
-                if i < NODE_TILES:
-                    gate_tile(s, i, gated)
-                if i > 0:
-                    nc.vector.tensor_reduce(
-                        out=neg_max[:, i - 1 : i], in_=gated[:, i - 1, :], axis=AX.X, op=ALU.max, negate=True
-                    )
-            live["gated", s], live["neg_max", s] = gated, neg_max
+        def top(s, first, count):
+            nc.vector.tensor_reduce(
+                out=live["neg_max", s][:, first : first + count],
+                in_=live["gated", s][:, first : first + count, :],
+                axis=AX.X,
+                op=ALU.max,
+                negate=True,
+            )
 
         def soften(s):
             e_rows = work.tile([P, NODE_TILES, NODES], BF16)
@@ -261,11 +240,25 @@ def tile_gatedspatialattentionlayer_pb_t_kernel(
                 )
             live["e_rows", s], live["row_sum", s] = e_rows, row_sum
 
+        def warm(bank, s):
+            if ("e_codes", s) in live:
+                nc.tensor.matmul_mx(
+                    out=bank,
+                    lhsT=live["e_codes", s][:, 0, :].bitcast(FP8X4),
+                    lhsT_scale=live["e_scales", s][:, 0, :],
+                    rhs=live["e_codes", s][:].rearrange("p i r -> p (i r)").bitcast(FP8X4),
+                    rhs_scale=live["e_scales", s][:].rearrange("p i r -> p (i r)"),
+                    start=True,
+                    stop=True,
+                )
+
         def flip_e(s):
             e_words = live["e_rows", s][:].bitcast(F32)
             e_grouped = work.tile([P, NODE_TILES, P, PACK], BF16, align_bytes=64, bufs=5)
             for b in range(NODE_TILES // 2):
-                e_flipped = psum.tile([P, 2, 2, P], F32, tag="e_flip", bufs=2)
+                e_flipped = psum.tile([P, 2, 2, P], F32, tag="words", bufs=2)
+                for n in range(0 if b == 0 else 0):
+                    warm(e_flipped[:].rearrange("p c u r -> p (c u r)"), s - 2)
                 for c in range(2):
                     for u in range(2):
                         nc.tensor.transpose(
@@ -309,17 +302,19 @@ def tile_gatedspatialattentionlayer_pb_t_kernel(
                 )
             live["o_sums", s] = o_sums
 
+        def squash(s, squashed, i):
+            nc.scalar.activation(
+                out=squashed[:, i, :],
+                in_=live["o_sums", s][:, i, :],
+                func=ACT.Tanh,
+                scale=live["inv_sum", s][:, i : i + 1],
+            )
+
         def finish(s):
-            t, h = s // HEADS, s % HEADS
             squashed = work.tile([P, NODE_TILES, HEAD_DIM], F32)
-            for i in range(NODE_TILES):
-                nc.scalar.activation(
-                    out=squashed[:, i, :],
-                    in_=live["o_sums", s][:, i, :],
-                    func=ACT.Tanh,
-                    scale=live["inv_sum", s][:, i : i + 1],
-                )
             result = work.tile([P, NODE_TILES, HEAD_DIM], F32, bufs=3)
+            for i in range(NODE_TILES):
+                squash(s, squashed, i)
             nc.gpsimd.tensor_tensor(out=result[:], in0=squashed[:], in1=live["h_rows", s][:], op=ALU.add)
             nc.gpsimd.tensor_scalar(
                 out=result[:], in0=result[:], scalar1=0.5, scalar2=0.0, op0=ALU.mult, op1=ALU.add
@@ -340,12 +335,7 @@ def tile_gatedspatialattentionlayer_pb_t_kernel(
             for b in range(2):
                 tiles = slice(2 * b, 2 * b + 2)
                 for i in range(2 * b, 2 * b + 2):
-                    nc.scalar.activation(
-                        out=squashed[:, i, :],
-                        in_=live["o_sums", s][:, i, :],
-                        func=ACT.Tanh,
-                        scale=live["inv_sum", s][:, i : i + 1],
-                    )
+                    squash(s, squashed, i)
                 nc.vector.scalar_tensor_tensor(
                     out=result[:, tiles, :],
                     in0=squashed[:, tiles, :],
@@ -372,14 +362,20 @@ def tile_gatedspatialattentionlayer_pb_t_kernel(
             if 0 <= s < SLICES:
                 stage(s)
 
+        def lag(j):
+            return 2 if j < SLICES - 4 else (SLICES - 1 - j) // 2
+
+        def turn(j):
+            return lag(j) + 2 if j < SLICES - 3 else 3
+
         def pack(s):
             for j in range(SLICES):
                 if j + lag(j) + 1 == s:
                     pack_v(j)
             run(pack_e, s - 2)
 
-        def lag(j):
-            return 3 - j // 6
+        def beside(j):
+            return False
 
         load_qk(0)
         load_gate(0)
@@ -396,70 +392,80 @@ def tile_gatedspatialattentionlayer_pb_t_kernel(
         load_w(1)
         flip_qk(0)
         keep_qk(0)
-        score(0)
+        for i in range(NODE_TILES):
+            score(0, i)
         flip_qk(1)
         keep_qk(1)
-        for s in range(SLICES + 3):
-            for j in range(LAST - 1):
-                if j + max(lag(j) + 2, 3) == s - 1:
-                    store(j)
-            run(load_qk, s + 3)
-            run(load_gate, s + 3)
+        load_qk(3)
+        load_gate(3)
+        load_qk(4)
+        for s in range(SLICES + 4):
+            values = [j for j in range(SLICES) if j + lag(j) == s]
+            done = [j for j in range(SLICES) if j + turn(j) == s]
+            run(load_qk, s + 5)
+            run(load_gate, s + 4)
             if s + 2 < HEADS:
                 load_w(s + 2)
-            run(load_h, s - 0)
+            run(load_h, s)
             ahead, part = (s + 6) // HEADS, (s + 6) % HEADS
             if 1 <= ahead < STEPS and part < NODE_TILES:
                 load_x(ahead, part)
-            values = [j for j in range(SLICES) if j + lag(j) == s]
-            done = [j for j in range(SLICES) if j + max(lag(j) + 2, 3) == s]
+            for j in range(SLICES - 2):
+                if j + turn(j) == s - 1:
+                    store(j)
             for j in done:
                 attend(j)
             if s >= LAST:
                 pack(s)
+            if s < LAST:
+                for i in range(NODE_TILES):
+                    gate(s, i)
             if s == LAST:
-                gate_last(s)
+                for i in range(NODE_TILES + 1):
+                    if i < NODE_TILES:
+                        gate(s, i)
+                    if i > 0:
+                        top(s, i - 1, 1)
                 halve_h(s - 1)
                 halve_h(s)
-            else:
-                run(gate, s)
             for j in values:
                 project_v(j)
-                if not (j % 2 == 1 and j < SLICES - 3):
+                if not beside(j):
                     bias_v(j)
-            run(score, s + 1)
-            if s != LAST:
-                run(top, s)
-            if 1 <= s <= 2:
-                for x in range(2 * s - 2, 2 * s):
-                    pack_x(0, x)
-            if 1 <= s < HEADS + 1:
-                pack_w(s - 1)
-            later, part = (s + 4) // HEADS, (s + 4) % HEADS - 1
-            if 1 <= later < STEPS and 0 <= part < NODE_TILES:
-                pack_x(later, part)
-            if s > LAST + 1:
-                for j in done:
+            for i in range(NODE_TILES):
+                score(s + 1, i)
+            for j in done:
+                if j >= SLICES - 2:
                     finish_last(j)
-            else:
-                for j in done:
+                else:
                     finish(j)
             for j in values:
-                if j % 2 == 1 and j < SLICES - 3:
+                if beside(j):
                     bias_v_beside(j)
-            if s != LAST + 1:
-                run(soften, s - 1)
-            if s == LAST + 1:
-                soften(LAST)
+            if s < LAST:
+                top(s, 0, NODE_TILES)
+            if s == 1:
+                for c in range(NODE_TILES):
+                    pack_x(0, c)
+            if 1 <= s < HEADS + 1:
+                pack_w(s - 1)
+            later, part = (s + 4) // HEADS, (s + 4) % HEADS
+            if 1 <= later < STEPS and 1 <= part <= NODE_TILES:
+                pack_x(later, part - 1)
+            run(soften, s - 1)
             run(flip_e, s - 1)
-            run(flip_qk, s + 2)
-            run(keep_qk, s + 2)
-            if s < 2:
-                for x in range(2 * s, 2 * s + 2):
-                    flip_x(0, x)
+            if s > 0:
+                run(flip_qk, s + 2)
+                run(keep_qk, s + 2)
+            if s == 0:
+                for c in range(NODE_TILES):
+                    flip_x(0, c)
             if s < HEADS:
                 flip_w(s)
-            if 1 <= later < STEPS and 0 <= part + 1 < NODE_TILES:
-                flip_x(later, part + 1)
+            if s == 0:
+                run(flip_qk, s + 2)
+                run(keep_qk, s + 2)
+            if 1 <= later < STEPS and part < NODE_TILES:
+                flip_x(later, part)
             if s < LAST:
                 pack(s)

@@ -105,7 +105,10 @@ def tile_gatedspatialattentionlayer_pb_t_kernel(
 
         def project_v(s):
             t, h = s // HEADS, s % HEADS
-            v_sums = psum.tile([P, PACK, HEAD_DIM], F32, tag="scores", bufs=4)
+            if beside(s):
+                v_sums = psum.tile([P, PACK, HEAD_DIM], F32, tag="sums")
+            else:
+                v_sums = psum.tile([P, PACK, HEAD_DIM], F32, tag="scores", bufs=4)
             for c in range(NODE_TILES):
                 place = 2 * (c % 2) + c // 2
                 for g in range(FEATURE_PASSES):
@@ -322,7 +325,7 @@ def tile_gatedspatialattentionlayer_pb_t_kernel(
             live["result", s] = result
 
         def halve_h(s):
-            h_half = work.tile([P, NODE_TILES, HEAD_DIM], F32)
+            h_half = work.tile([P, NODE_TILES, HEAD_DIM], F32, bufs=3)
             nc.gpsimd.tensor_scalar(
                 out=h_half[:], in0=live["h_rows", s][:], scalar1=0.5, scalar2=0.0, op0=ALU.mult, op1=ALU.add
             )
@@ -375,18 +378,18 @@ def tile_gatedspatialattentionlayer_pb_t_kernel(
             run(pack_e, s - 2)
 
         def beside(j):
-            return False
+            return j % 2 == 1 and j < SLICES - 3
 
         load_qk(0)
         load_gate(0)
         load_qk(1)
         load_x(0, 0)
         load_x(0, 1)
+        load_qk(2)
         load_gate(1)
         load_x(0, 2)
         load_x(0, 3)
         load_w(0)
-        load_qk(2)
         load_gate(2)
         load_bias()
         load_w(1)
@@ -410,7 +413,7 @@ def tile_gatedspatialattentionlayer_pb_t_kernel(
             ahead, part = (s + 6) // HEADS, (s + 6) % HEADS
             if 1 <= ahead < STEPS and part < NODE_TILES:
                 load_x(ahead, part)
-            for j in range(SLICES - 2):
+            for j in range(SLICES - 3):
                 if j + turn(j) == s - 1:
                     store(j)
             for j in done:
@@ -426,22 +429,21 @@ def tile_gatedspatialattentionlayer_pb_t_kernel(
                         gate(s, i)
                     if i > 0:
                         top(s, i - 1, 1)
-                halve_h(s - 1)
-                halve_h(s)
+                for j in range(SLICES - 3, SLICES):
+                    halve_h(j)
             for j in values:
-                project_v(j)
                 if not beside(j):
+                    project_v(j)
                     bias_v(j)
             for i in range(NODE_TILES):
                 score(s + 1, i)
+            if s == LAST + 1:
+                soften(LAST)
             for j in done:
-                if j >= SLICES - 2:
+                if j >= SLICES - 3:
                     finish_last(j)
                 else:
                     finish(j)
-            for j in values:
-                if beside(j):
-                    bias_v_beside(j)
             if s < LAST:
                 top(s, 0, NODE_TILES)
             if s == 1:
@@ -452,19 +454,25 @@ def tile_gatedspatialattentionlayer_pb_t_kernel(
             later, part = (s + 4) // HEADS, (s + 4) % HEADS
             if 1 <= later < STEPS and 1 <= part <= NODE_TILES:
                 pack_x(later, part - 1)
-            run(soften, s - 1)
+            if s != LAST + 1:
+                run(soften, s - 1)
+            for j in values:
+                if beside(j):
+                    project_v(j)
+                    bias_v_beside(j)
             run(flip_e, s - 1)
             if s > 0:
                 run(flip_qk, s + 2)
                 run(keep_qk, s + 2)
             if s == 0:
-                for c in range(NODE_TILES):
-                    flip_x(0, c)
+                flip_x(0, 0)
+                flip_x(0, 1)
+                flip_qk(2)
+                keep_qk(2)
+                flip_x(0, 2)
+                flip_x(0, 3)
             if s < HEADS:
                 flip_w(s)
-            if s == 0:
-                run(flip_qk, s + 2)
-                run(keep_qk, s + 2)
             if 1 <= later < STEPS and part < NODE_TILES:
                 flip_x(later, part)
             if s < LAST:

@@ -260,8 +260,6 @@ def tile_gatedspatialattentionlayer_pb_t_kernel(
             e_grouped = work.tile([P, NODE_TILES, P, PACK], BF16, align_bytes=64, bufs=5)
             for b in range(NODE_TILES // 2):
                 e_flipped = psum.tile([P, 2, 2, P], F32, tag="words", bufs=2)
-                for n in range(0 if b == 0 else 0):
-                    warm(e_flipped[:].rearrange("p c u r -> p (c u r)"), s - 2)
                 for c in range(2):
                     for u in range(2):
                         nc.tensor.transpose(
@@ -269,6 +267,7 @@ def tile_gatedspatialattentionlayer_pb_t_kernel(
                             in_=e_words[:, 2 * b + c, u * P : (u + 1) * P],
                             identity=ident_f32[:],
                         )
+                    score(s + 2, 2 * b + c)
                 copy = nc.vector.tensor_copy if s == LAST and b == 1 else nc.scalar.copy
                 copy(
                     out=e_grouped[:, 2 * b : 2 * b + 2].bitcast(F32),
@@ -276,9 +275,12 @@ def tile_gatedspatialattentionlayer_pb_t_kernel(
                 )
             live["e_grouped", s] = e_grouped
 
-        def pack_e(s):
+        def invert(s):
             inv_sum = work.tile([P, NODE_TILES], F32, bufs=5)
             nc.vector.reciprocal(out=inv_sum[:], in_=live["row_sum", s][:])
+            live["inv_sum", s] = inv_sum
+
+        def pack_e(s):
             e_codes = work.tile([P, NODE_TILES, P], U32, align_bytes=64, bufs=5)
             e_scales = work.tile([P, NODE_TILES, P], U8, align_bytes=64, bufs=5)
             width = NODE_TILES // 2 if s == LAST else NODE_TILES
@@ -289,7 +291,7 @@ def tile_gatedspatialattentionlayer_pb_t_kernel(
                     scales=e_scales[:, tiles].rearrange("p i r -> p (i r)"),
                     in_=live["e_grouped", s][:, tiles].rearrange("p i r j -> p (i r j)"),
                 )
-            live["inv_sum", s], live["e_codes", s], live["e_scales", s] = inv_sum, e_codes, e_scales
+            live["e_codes", s], live["e_scales", s] = e_codes, e_scales
 
         def attend(s):
             o_sums = psum.tile([P, NODE_TILES, HEAD_DIM], F32, tag="sums")
@@ -375,6 +377,8 @@ def tile_gatedspatialattentionlayer_pb_t_kernel(
             for j in range(SLICES):
                 if j + lag(j) + 1 == s:
                     pack_v(j)
+            if s >= LAST:
+                run(invert, s - 2)
             run(pack_e, s - 2)
 
         def beside(j):
@@ -385,10 +389,10 @@ def tile_gatedspatialattentionlayer_pb_t_kernel(
         load_qk(1)
         load_x(0, 0)
         load_x(0, 1)
-        load_qk(2)
-        load_gate(1)
         load_x(0, 2)
+        load_qk(2)
         load_x(0, 3)
+        load_gate(1)
         load_w(0)
         load_gate(2)
         load_bias()
@@ -423,6 +427,7 @@ def tile_gatedspatialattentionlayer_pb_t_kernel(
             if s < LAST:
                 for i in range(NODE_TILES):
                     gate(s, i)
+                run(invert, s - 2)
             if s == LAST:
                 for i in range(NODE_TILES + 1):
                     if i < NODE_TILES:
@@ -435,8 +440,11 @@ def tile_gatedspatialattentionlayer_pb_t_kernel(
                 if not beside(j):
                     project_v(j)
                     bias_v(j)
-            for i in range(NODE_TILES):
-                score(s + 1, i)
+            if s == 0:
+                flip_x(0, 0)
+                flip_x(0, 1)
+                for i in range(NODE_TILES):
+                    score(1, i)
             if s == LAST + 1:
                 soften(LAST)
             for j in done:
@@ -465,8 +473,6 @@ def tile_gatedspatialattentionlayer_pb_t_kernel(
                 run(flip_qk, s + 2)
                 run(keep_qk, s + 2)
             if s == 0:
-                flip_x(0, 0)
-                flip_x(0, 1)
                 flip_qk(2)
                 keep_qk(2)
                 flip_x(0, 2)

@@ -467,8 +467,10 @@ def tile_gatedspatialattentionlayer_pb_t_kernel(
             for j in values:
                 if beside(j):
                     project_v(j)
-                    bias_v_beside(j)
             run(flip_e, s - 1)
+            for j in values:
+                if beside(j):
+                    bias_v_beside(j)
             if s > 0:
                 run(flip_qk, s + 2)
                 run(keep_qk, s + 2)

from contextlib import ExitStack
import math

import concourse.mybir as mybir
from concourse.masks import make_identity

F32 = mybir.dt.float32
BF16 = mybir.dt.bfloat16
U32 = mybir.dt.uint32
U8 = mybir.dt.uint8
FP8X4 = mybir.dt.float8_e4m3fn_x4
ALU = mybir.AluOpType
ACT = mybir.ActivationFunctionType
AX = mybir.AxisListType

P = 128
PACK = 4
STEPS = 3
HEADS = 8
NODES = 512
FEATURES = 1024
HEAD_DIM = FEATURES // HEADS
NODE_TILES = NODES // P
FEATURE_PASSES = FEATURES // (P * PACK)
SCORE_SCALE = 1.0 / math.sqrt(HEAD_DIM)

FLOPS = 2 * STEPS * NODES * FEATURES * FEATURES + 2 * (2 * STEPS * HEADS * NODES * NODES * HEAD_DIM)

SLICES = STEPS * HEADS
LAST = SLICES - 1


def tile_gatedspatialattentionlayer_pb_t_kernel(
    tc, q_heads, k_heads, value, Wv, bv, dyn, h_gcn, out
):
    nc = tc.nc
    with ExitStack() as ctx:
        ctx.enter_context(tc.manual_schedule())
        const = ctx.enter_context(tc.tile_pool(name="const", bufs=1))
        project = ctx.enter_context(tc.tile_pool(name="project", bufs=2))
        loads = ctx.enter_context(tc.tile_pool(name="loads", bufs=3))
        work = ctx.enter_context(tc.tile_pool(name="work", bufs=2))
        psum = ctx.enter_context(tc.psum_pool(name="psum", bufs=1))

        ident_bf16 = const.tile([P, P], BF16)
        make_identity(nc, ident_bf16[:])
        ident_f32 = const.tile([P, P], F32)
        make_identity(nc, ident_f32[:])
        bias_rows = const.tile([P, FEATURES], BF16)
        w_codes = const.tile([P, HEADS, FEATURE_PASSES, P], U32, align_bytes=64)
        w_scales = const.tile([P, HEADS, FEATURE_PASSES, P], U8, align_bytes=64)

        live = {}

        def load_bias():
            nc.sync.dma_start(out=bias_rows[:], in_=bv.partition_broadcast(P))

        def load_w(h):
            w_rows = project.tile([P, FEATURES], BF16, bufs=3)
            nc.sync.dma_start(out=w_rows[:], in_=Wv[h * P : (h + 1) * P, :])
            live["w_rows", h] = w_rows

        def load_x(t, c):
            x_rows = project.tile([P, FEATURES], BF16, bufs=5)
            nc.sync.dma_start(out=x_rows[:], in_=value[0, t].rearrange("(p c) f -> p c f", c=NODE_TILES)[:, c, :])
            live["x_rows", t, c] = x_rows

        def features_to_partitions(rows, grouped):
            words = rows.bitcast(F32)
            flipped = psum.tile([P, FEATURE_PASSES, 2, P], F32, tag="words", bufs=2)
            for g in range(FEATURE_PASSES):
                for u in range(2):
                    first = (2 * g + u) * P
                    nc.tensor.transpose(
                        out=flipped[:, g, u, :], in_=words[:, first : first + P], identity=ident_f32[:]
                    )
            nc.scalar.copy(out=grouped.bitcast(F32), in_=flipped[:].rearrange("p g u r -> p g r u"))

        def flip_w(h):
            w_grouped = project.tile([P, FEATURE_PASSES, P, PACK], BF16, align_bytes=64, bufs=3)
            features_to_partitions(live["w_rows", h][:], w_grouped[:])
            live["w_grouped", h] = w_grouped

        def pack_w(h):
            nc.vector.quantize_mx(
                out=w_codes[:, h].rearrange("p g r -> p (g r)").bitcast(FP8X4),
                scales=w_scales[:, h].rearrange("p g r -> p (g r)"),
                in_=live["w_grouped", h][:].rearrange("p g r j -> p (g r j)"),
            )

        def flip_x(t, c):
            x_grouped = project.tile([P, FEATURE_PASSES, P, PACK], BF16, align_bytes=64, bufs=5)
            features_to_partitions(live["x_rows", t, c][:], x_grouped[:])
            live["x_grouped", t, c] = x_grouped

        def pack_x(t, c):
            x_codes = project.tile([P, FEATURE_PASSES, P], U32, align_bytes=64, bufs=2 * NODE_TILES)
            x_scales = project.tile([P, FEATURE_PASSES, P], U8, align_bytes=64, bufs=2 * NODE_TILES)
            nc.vector.quantize_mx(
                out=x_codes[:].rearrange("p g r -> p (g r)").bitcast(FP8X4),
                scales=x_scales[:].rearrange("p g r -> p (g r)"),
                in_=live["x_grouped", t, c][:].rearrange("p g r j -> p (g r j)"),
            )
            live["x_codes", t, c], live["x_scales", t, c] = x_codes, x_scales

        def project_v(s):
            t, h = s // HEADS, s % HEADS
            if beside(s):
                v_sums = psum.tile([P, PACK, HEAD_DIM], F32, tag="sums")
            else:
                v_sums = psum.tile([P, PACK, HEAD_DIM], F32, tag="scores", bufs=4)
            for c in range(NODE_TILES):
                place = 2 * (c % 2) + c // 2
                for g in range(FEATURE_PASSES):
                    nc.tensor.matmul_mx(
                        out=v_sums[:, place, :],
                        lhsT=live["x_codes", t, c][:, g, :].bitcast(FP8X4),
                        lhsT_scale=live["x_scales", t, c][:, g, :],
                        rhs=w_codes[:, h, g, :].bitcast(FP8X4),
                        rhs_scale=w_scales[:, h, g, :],
                        start=(g == 0),
                        stop=(g == FEATURE_PASSES - 1),
                    )
            live["v_sums", s] = v_sums

        def bias_of(s):
            h = s % HEADS
            row = bias_rows[:, h * HEAD_DIM : (h + 1) * HEAD_DIM]
            return row.unsqueeze(2).to_broadcast([P, HEAD_DIM, PACK])

        def bias_v(s):
            v_grouped = project.tile([P, HEAD_DIM, PACK], BF16, align_bytes=64, bufs=4)
            nc.vector.tensor_tensor(
                out=v_grouped[:], in0=live["v_sums", s][:].rearrange("p j d -> p d j"), in1=bias_of(s), op=ALU.add
            )
            live["v_grouped", s] = v_grouped

        def bias_v_beside(s):
            v_plain = project.tile([P, HEAD_DIM, PACK], F32)
            nc.scalar.copy(out=v_plain[:], in_=live["v_sums", s][:].rearrange("p j d -> p d j"))
            v_grouped = project.tile([P, HEAD_DIM, PACK], BF16, align_bytes=64, bufs=4)
            nc.gpsimd.tensor_tensor(out=v_grouped[:], in0=v_plain[:], in1=bias_of(s), op=ALU.add)
            live["v_grouped", s] = v_grouped

        def pack_v(s):
            v_codes = project.tile([P, HEAD_DIM], U32, align_bytes=64, bufs=5)
            v_scales = project.tile([P, HEAD_DIM], U8, align_bytes=64, bufs=5)
            nc.vector.quantize_mx(
                out=v_codes[:].bitcast(FP8X4),
                scales=v_scales[:],
                in_=live["v_grouped", s][:].rearrange("p d j -> p (d j)"),
            )
            live["v_codes", s], live["v_scales", s] = v_codes, v_scales

        def load_qk(s):
            t, h = s // HEADS, s % HEADS
            q_rows = loads.tile([P, NODE_TILES, HEAD_DIM], BF16, bufs=5)
            nc.sync.dma_start(out=q_rows[:], in_=q_heads[h, t].rearrange("(p i) d -> p i d", i=NODE_TILES))
            k_rows = loads.tile([P, 2, 2, HEAD_DIM], BF16, bufs=5)
            nc.sync.dma_start(out=k_rows[:], in_=k_heads[h, t].rearrange("(a p u) d -> p a u d", a=2, u=2))
            live["q_rows", s], live["k_rows", s] = q_rows, k_rows

        def load_gate(s):
            t, h = s // HEADS, s % HEADS
            dyn_rows = loads.tile([P, NODE_TILES, NODES], BF16, bufs=6)
            nc.sync.dma_start(out=dyn_rows[:], in_=dyn[h, t].rearrange("(p i) m -> p i m", i=NODE_TILES))
            live["dyn_rows", s] = dyn_rows

        def load_h(s):
            t, h = s // HEADS, s % HEADS
            h_rows = loads.tile([P, NODE_TILES, HEAD_DIM], BF16, bufs=8)
            nc.sync.dma_start(
                out=h_rows[:],
                in_=h_gcn[0, t].rearrange("(p i) f -> p i f", i=NODE_TILES)[:, :, h * HEAD_DIM : (h + 1) * HEAD_DIM],
            )
            live["h_rows", s] = h_rows

        def flip_qk(s):
            qk_flipped = psum.tile([P, 2 * NODE_TILES, P], BF16, tag="flip")
            for i in range(NODE_TILES):
                nc.tensor.transpose(out=qk_flipped[:, i, :], in_=live["q_rows", s][:, i, :], identity=ident_bf16[:])
            for u in range(2):
                for a in range(2):
                    nc.tensor.transpose(
                        out=qk_flipped[:, NODE_TILES + 2 * u + a, :],
                        in_=live["k_rows", s][:, a, u, :],
                        identity=ident_bf16[:],
                    )
            live["qk_flipped", s] = qk_flipped

        def keep_qk(s):
            qk_t = work.tile([P, 2 * NODE_TILES, P], BF16, bufs=3)
            nc.scalar.copy(out=qk_t[:], in_=live["qk_flipped", s][:])
            live["qk_t", s] = qk_t

        def score(s, i):
            if s < SLICES:
                qk_t = live["qk_t", s]
                scores = psum.tile([P, NODES], F32, tag="scores", bufs=4)
                nc.tensor.matmul(
                    out=scores[:],
                    lhsT=qk_t[:, i, :],
                    rhs=qk_t[:, NODE_TILES:, :].rearrange("p j c -> p (j c)"),
                    start=True,
                    stop=True,
                )
                live["scores", s, i] = scores

        def gate(s, i):
            if i == 0:
                gated = work.tile([P, NODE_TILES, NODES], F32)
                neg_max = work.tile([P, NODE_TILES], F32)
                live["gated", s], live["neg_max", s] = gated, neg_max
            nc.vector.scalar_tensor_tensor(
                out=live["gated", s][:, i, :].rearrange("p (u y) -> p u y", u=2),
                in0=live["scores", s, i][:].rearrange("p (u y) -> p u y", u=2),
                scalar=SCORE_SCALE,
                in1=live["dyn_rows", s][:, i, :].rearrange("p (y u) -> p u y", u=2),
                op0=ALU.mult,
                op1=ALU.mult,
            )

        def top(s, first, count):
            nc.vector.tensor_reduce(
                out=live["neg_max", s][:, first : first + count],
                in_=live["gated", s][:, first : first + count, :],
                axis=AX.X,
                op=ALU.max,
                negate=True,
            )

        def soften(s):
            e_rows = work.tile([P, NODE_TILES, NODES], BF16)
            row_sum = work.tile([P, NODE_TILES], F32, bufs=5)
            for i in range(NODE_TILES):
                nc.scalar.activation(
                    out=e_rows[:, i, :],
                    in_=live["gated", s][:, i, :],
                    func=ACT.Exp,
                    bias=live["neg_max", s][:, i : i + 1],
                    scale=1.0,
                    accum_out=row_sum[:, i : i + 1],
                )
            live["e_rows", s], live["row_sum", s] = e_rows, row_sum

        def warm(bank, s):
            if ("e_codes", s) in live:
                nc.tensor.matmul_mx(
                    out=bank,
                    lhsT=live["e_codes", s][:, 0, :].bitcast(FP8X4),
                    lhsT_scale=live["e_scales", s][:, 0, :],
                    rhs=live["e_codes", s][:].rearrange("p i r -> p (i r)").bitcast(FP8X4),
                    rhs_scale=live["e_scales", s][:].rearrange("p i r -> p (i r)"),
                    start=True,
                    stop=True,
                )

        def flip_e(s):
            e_words = live["e_rows", s][:].bitcast(F32)
            e_grouped = work.tile([P, NODE_TILES, P, PACK], BF16, align_bytes=64, bufs=5)
            for b in range(NODE_TILES // 2):
                e_flipped = psum.tile([P, 2, 2, P], F32, tag="words", bufs=2)
                for c in range(2):
                    for u in range(2):
                        nc.tensor.transpose(
                            out=e_flipped[:, c, u, :],
                            in_=e_words[:, 2 * b + c, u * P : (u + 1) * P],
                            identity=ident_f32[:],
                        )
                    score(s + 2, 2 * b + c)
                copy = nc.vector.tensor_copy if s == LAST and b == 1 else nc.scalar.copy
                copy(
                    out=e_grouped[:, 2 * b : 2 * b + 2].bitcast(F32),
                    in_=e_flipped[:].rearrange("p c u r -> p c r u"),
                )
            live["e_grouped", s] = e_grouped

        def invert(s):
            inv_sum = work.tile([P, NODE_TILES], F32, bufs=5)
            nc.vector.reciprocal(out=inv_sum[:], in_=live["row_sum", s][:])
            live["inv_sum", s] = inv_sum

        def pack_e(s):
            e_codes = work.tile([P, NODE_TILES, P], U32, align_bytes=64, bufs=5)
            e_scales = work.tile([P, NODE_TILES, P], U8, align_bytes=64, bufs=5)
            width = NODE_TILES // 2 if s == LAST else NODE_TILES
            for i in range(0, NODE_TILES, width):
                tiles = slice(i, i + width)
                nc.vector.quantize_mx(
                    out=e_codes[:, tiles].rearrange("p i r -> p (i r)").bitcast(FP8X4),
                    scales=e_scales[:, tiles].rearrange("p i r -> p (i r)"),
                    in_=live["e_grouped", s][:, tiles].rearrange("p i r j -> p (i r j)"),
                )
            live["e_codes", s], live["e_scales", s] = e_codes, e_scales

        def attend(s):
            o_sums = psum.tile([P, NODE_TILES, HEAD_DIM], F32, tag="sums")
            for i in range(NODE_TILES):
                nc.tensor.matmul_mx(
                    out=o_sums[:, i, :],
                    lhsT=live["e_codes", s][:, i, :].bitcast(FP8X4),
                    lhsT_scale=live["e_scales", s][:, i, :],
                    rhs=live["v_codes", s][:].bitcast(FP8X4),
                    rhs_scale=live["v_scales", s][:],
                    start=True,
                    stop=True,
                )
            live["o_sums", s] = o_sums

        def squash(s, squashed, i):
            nc.scalar.activation(
                out=squashed[:, i, :],
                in_=live["o_sums", s][:, i, :],
                func=ACT.Tanh,
                scale=live["inv_sum", s][:, i : i + 1],
            )

        def finish(s):
            squashed = work.tile([P, NODE_TILES, HEAD_DIM], F32)
            result = work.tile([P, NODE_TILES, HEAD_DIM], F32, bufs=3)
            for i in range(NODE_TILES):
                squash(s, squashed, i)
            nc.gpsimd.tensor_tensor(out=result[:], in0=squashed[:], in1=live["h_rows", s][:], op=ALU.add)
            nc.gpsimd.tensor_scalar(
                out=result[:], in0=result[:], scalar1=0.5, scalar2=0.0, op0=ALU.mult, op1=ALU.add
            )
            live["result", s] = result

        def halve_h(s):
            h_half = work.tile([P, NODE_TILES, HEAD_DIM], F32, bufs=3)
            nc.gpsimd.tensor_scalar(
                out=h_half[:], in0=live["h_rows", s][:], scalar1=0.5, scalar2=0.0, op0=ALU.mult, op1=ALU.add
            )
            live["h_half", s] = h_half

        def finish_last(s):
            t, h = s // HEADS, s % HEADS
            squashed = work.tile([P, NODE_TILES, HEAD_DIM], F32)
            result = work.tile([P, NODE_TILES, HEAD_DIM], F32, bufs=3)
            for b in range(2):
                tiles = slice(2 * b, 2 * b + 2)
                for i in range(2 * b, 2 * b + 2):
                    squash(s, squashed, i)
                nc.vector.scalar_tensor_tensor(
                    out=result[:, tiles, :],
                    in0=squashed[:, tiles, :],
                    scalar=0.5,
                    in1=live["h_half", s][:, tiles, :],
                    op0=ALU.mult,
                    op1=ALU.add,
                )
                nc.sync.dma_start(
                    out=out[0, t].rearrange("(p i) f -> p i f", i=NODE_TILES)[
                        :, tiles, h * HEAD_DIM : (h + 1) * HEAD_DIM
                    ],
                    in_=result[:, tiles, :],
                )

        def store(s):
            t, h = s // HEADS, s % HEADS
            nc.sync.dma_start(
                out=out[0, t].rearrange("(p i) f -> p i f", i=NODE_TILES)[:, :, h * HEAD_DIM : (h + 1) * HEAD_DIM],
                in_=live["result", s][:],
            )

        def run(stage, s):
            if 0 <= s < SLICES:
                stage(s)

        def lag(j):
            return 2 if j < SLICES - 4 else (SLICES - 1 - j) // 2

        def turn(j):
            return lag(j) + 2 if j < SLICES - 3 else 3

        def pack(s):
            for j in range(SLICES):
                if j + lag(j) + 1 == s:
                    pack_v(j)
            if s >= LAST:
                run(invert, s - 2)
            run(pack_e, s - 2)

        def beside(j):
            return j % 2 == 1 and j < SLICES - 3

        load_qk(0)
        load_gate(0)
        load_qk(1)
        load_x(0, 0)
        load_x(0, 1)
        load_x(0, 2)
        load_qk(2)
        load_x(0, 3)
        load_gate(1)
        load_w(0)
        load_gate(2)
        load_bias()
        load_w(1)
        flip_qk(0)
        keep_qk(0)
        for i in range(NODE_TILES):
            score(0, i)
        flip_qk(1)
        keep_qk(1)
        load_qk(3)
        load_gate(3)
        load_qk(4)
        for s in range(SLICES + 4):
            values = [j for j in range(SLICES) if j + lag(j) == s]
            done = [j for j in range(SLICES) if j + turn(j) == s]
            run(load_qk, s + 5)
            run(load_gate, s + 4)
            if s + 2 < HEADS:
                load_w(s + 2)
            run(load_h, s)
            ahead, part = (s + 6) // HEADS, (s + 6) % HEADS
            if 1 <= ahead < STEPS and part < NODE_TILES:
                load_x(ahead, part)
            for j in range(SLICES - 3):
                if j + turn(j) == s - 1:
                    store(j)
            for j in done:
                attend(j)
            if s >= LAST:
                pack(s)
            if s < LAST:
                for i in range(NODE_TILES):
                    gate(s, i)
                run(invert, s - 2)
            if s == LAST:
                for i in range(NODE_TILES + 1):
                    if i < NODE_TILES:
                        gate(s, i)
                    if i > 0:
                        top(s, i - 1, 1)
                for j in range(SLICES - 3, SLICES):
                    halve_h(j)
            for j in values:
                if not beside(j):
                    project_v(j)
                    bias_v(j)
            if s == 0:
                flip_x(0, 0)
                flip_x(0, 1)
                for i in range(NODE_TILES):
                    score(1, i)
            if s == LAST + 1:
                soften(LAST)
            for j in done:
                if j >= SLICES - 3:
                    finish_last(j)
                else:
                    finish(j)
            if s < LAST:
                top(s, 0, NODE_TILES)
            if s == 1:
                for c in range(NODE_TILES):
                    pack_x(0, c)
            if 1 <= s < HEADS + 1:
                pack_w(s - 1)
            later, part = (s + 4) // HEADS, (s + 4) % HEADS
            if 1 <= later < STEPS and 1 <= part <= NODE_TILES:
                pack_x(later, part - 1)
            if s != LAST + 1:
                run(soften, s - 1)
            for j in values:
                if beside(j):
                    project_v(j)
            run(flip_e, s - 1)
            for j in values:
                if beside(j):
                    bias_v_beside(j)
            if s > 0:
                run(flip_qk, s + 2)
                run(keep_qk, s + 2)
            if s == 0:
                flip_qk(2)
                keep_qk(2)
                flip_x(0, 2)
                flip_x(0, 3)
            if s < HEADS:
                flip_w(s)
            if 1 <= later < STEPS and part < NODE_TILES:
                flip_x(later, part)
            if s < LAST:
                pack(s)
